import numpy as np
import ml_dtypes


def mxq(x, axis, fmt="e4m3"):
    dtype, down = {"e4m3": (ml_dtypes.float8_e4m3fn, 7), "e5m2": (ml_dtypes.float8_e5m2, 14)}[fmt]
    v = np.moveaxis(np.asarray(x, np.float32).astype(ml_dtypes.bfloat16).astype(np.float64), axis, -1)
    blocks = v.reshape(v.shape[:-1] + (-1, 32))
    amax = np.abs(blocks).max(-1, keepdims=True)
    byte = np.maximum(np.where(amax > 0, np.frexp(amax)[1] - 1 + 127, 0) - down, 1)
    scale = np.exp2(byte - 127.0)
    codes = (blocks / scale).astype(np.float32).astype(dtype).astype(np.float64)
    return np.moveaxis((codes * scale).reshape(v.shape), -1, axis)


WIDE = False


def mx_kscale(k):
    if not WIDE:
        return np.ones(k)
    levels = np.array([10, -10, 5, -5, 0])
    if k % 512:
        return np.exp2(np.random.permutation(np.resize(levels, k // 32))).repeat(32)
    a = np.empty((k // 512, 16))
    for p in range(k // 512):
        a[p, :8] = np.random.permutation(np.resize(levels, 8))
        for g in range(8):
            far = levels[np.abs(levels - a[p, g]) >= 10]
            a[p, g + 8] = far[np.random.randint(len(far))]
    return np.exp2(a.ravel()).repeat(32)


BF16 = ml_dtypes.bfloat16


def bf(x):
    return np.asarray(x, np.float32).astype(BF16)


def f64(x):
    return np.asarray(x).astype(np.float64)


B, L, C, H, BLK = 8, 512, 512, 8, 128
D = C // H
MAX_SCALE_MUL = np.log(100.0)
EPS = 1e-12


def l2norm(t):
    n = np.sqrt(np.sum(t * t, axis=-1, keepdims=True))
    return t / np.maximum(n, EPS)


def setup_inputs():
    s = mx_kscale(C)
    lsm = np.linspace(np.log(4.0), MAX_SCALE_MUL + 1.0, H) + 0.05 * np.random.standard_normal(H)
    return {"x": bf(np.random.standard_normal((B, L, C)) * s),
            "W_qkv": bf(np.random.standard_normal((3 * C, C)) / np.sqrt(C) / s[None, :]),
            "q_bias": bf(np.random.standard_normal(C) * 0.3),
            "v_bias": bf(np.random.standard_normal(C) * 0.3),
            "log_scale_mul": bf(lsm.reshape(1, H, 1, 1))}


def reference(x, W_qkv, q_bias, v_bias, log_scale_mul):
    qb = f64(q_bias)
    bias = np.concatenate([qb, np.zeros_like(qb), f64(v_bias)])
    qkv = (mxq(f64(x), 2, "e4m3") @ mxq(f64(W_qkv), 1, "e4m3").T) + bias
    qkv = qkv.reshape(B, L, 3, H, D)
    q, k, v = np.moveaxis(qkv, 2, 0)
    q = np.swapaxes(q, 1, 2)
    k = np.swapaxes(k, 1, 2)
    v = np.swapaxes(v, 1, 2)
    scale_mul = np.exp(np.minimum(f64(log_scale_mul), MAX_SCALE_MUL))
    q = l2norm(q) * scale_mul
    k = l2norm(k)
    return q, k, v

@@ -1,0 +1,281 @@
+import math
+from contextlib import ExitStack
+
+import concourse.mybir as mybir
+from concourse.masks import make_identity
+
+F32 = mybir.dt.float32
+BF16 = mybir.dt.bfloat16
+U32 = mybir.dt.uint32
+U8 = mybir.dt.uint8
+FP8X4 = mybir.dt.float8_e4m3fn_x4
+ALU = mybir.AluOpType
+ACT = mybir.ActivationFunctionType
+AXIS = mybir.AxisListType
+
+P = 128
+BATCHES, TOKENS, FEATURES, HEADS = 8, 512, 512, 8
+HEAD_DIM = FEATURES // HEADS
+WORDS = FEATURES // 2
+PARTS = 3
+Q, K, V = 0, 1, 2
+MAX_LOG_MUL = math.log(100.0)
+EPS = 1e-12
+
+GROUP_BATCHES = 2
+GROUPS = BATCHES // GROUP_BATCHES
+RUN = GROUP_BATCHES * TOKENS // P
+N_TILES = GROUPS * RUN
+PART_TILES = FEATURES // P
+AHEAD = 4
+LAG = 3
+N_STEPS = N_TILES + (PARTS - 1) * LAG
+
+FLOPS = 2 * BATCHES * TOKENS * FEATURES * PARTS * FEATURES
+
+
+def tile_selfattention_pa_t_kernel(
+    tc, x, w_qkv, q_bias, v_bias, log_scale_mul, out_q, out_k, out_v
+):
+    nc = tc.nc
+    outs = [out_q, out_k, out_v]
+    with ExitStack() as ctx:
+        ctx.enter_context(tc.manual_schedule())
+        keep = ctx.enter_context(tc.tile_pool(name="keep", bufs=1))
+        work = ctx.enter_context(tc.tile_pool(name="work", bufs=3))
+        small = ctx.enter_context(tc.tile_pool(name="small", bufs=4))
+        stage = ctx.enter_context(tc.tile_pool(name="stage", bufs=2))
+        psum = ctx.enter_context(tc.psum_pool(name="psum", bufs=1))
+        banks = {"flipped": 2, "acc0": 2, "acc1": 3, "acc2": 1}
+
+        w_raw = keep.tile([P, PARTS * PART_TILES * FEATURES], BF16, name="w_raw")
+        x_raw = [keep.tile([P, RUN * FEATURES], BF16, name="x_raw%d" % g) for g in range(GROUPS)]
+        rows = keep.tile([P, 2 * FEATURES + 64], BF16, name="rows")
+        nc.vector.memset(rows[:], 0.0)
+        nc.scalar.dma_start(out=rows[0:1, 0:FEATURES], in_=q_bias.rearrange("(o n) -> o n", o=1))
+        nc.scalar.dma_start(out=rows[0:1, FEATURES : 2 * FEATURES], in_=v_bias.rearrange("(o n) -> o n", o=1))
+        nc.scalar.dma_start(
+            out=rows[0:1, 2 * FEATURES : 2 * FEATURES + HEADS],
+            in_=log_scale_mul.rearrange("a h b c -> a (h b c)"),
+        )
+
+        def load_w(part):
+            nc.sync.dma_start(
+                out=w_raw[:, part * PART_TILES * FEATURES : (part + 1) * PART_TILES * FEATURES].rearrange(
+                    "p (n f) -> p n f", n=PART_TILES
+                ),
+                in_=w_qkv[part * FEATURES : (part + 1) * FEATURES, :].rearrange("(n p) f -> p n f", p=P),
+            )
+
+        def load_x(g):
+            for j in range(GROUP_BATCHES):
+                nc.sync.dma_start(
+                    out=x_raw[g][j:P:GROUP_BATCHES, :],
+                    in_=x[g * GROUP_BATCHES + j].rearrange("(c t) f -> c (t f)", t=RUN),
+                )
+
+        load_w(Q)
+        load_x(0)
+        load_w(K)
+        load_w(V)
+        for g in range(1, GROUPS):
+            load_x(g)
+
+        ident = keep.tile([P, P], F32, name="ident")
+        make_identity(nc, ident[:])
+        ones = keep.tile([P, P], BF16, name="ones")
+        nc.vector.memset(ones[:], 1.0)
+        shrink = keep.tile([P, 2 * HEADS], F32, name="shrink")
+        nc.vector.memset(shrink[:, HEADS : 2 * HEADS], 1.0)
+
+        w_words = keep.tile([P, PARTS * FEATURES], U32, name="w_words", align_bytes=64)
+        w_scales = keep.tile([P, PARTS * FEATURES], U8, name="w_scales", align_bytes=64)
+        x_words = keep.tile([P, N_TILES * P], U32, name="x_words", align_bytes=64)
+        x_scales = keep.tile([P, N_TILES * P], U8, name="x_scales", align_bytes=64)
+
+        def flip(raw_words):
+            flipped = psum.tile([P, 4 * P], F32, tag="flipped", bufs=banks["flipped"])
+            for piece in range(4):
+                cols = slice(piece * P, (piece + 1) * P)
+                j, u = divmod(piece, 2)
+                nc.tensor.transpose(flipped[:, cols], raw_words[:, j * WORDS + u : (j + 1) * WORDS : 2], ident[:])
+            return flipped
+
+        def regroup(flipped):
+            grouped = work.tile([P, 8 * P], BF16, tag="grouped", align_bytes=64)
+            nc.scalar.copy(
+                out=grouped[:].bitcast(F32).rearrange("p (j r u) -> p j r u", j=2, u=2),
+                in_=flipped[:].rearrange("p (j u r) -> p j r u", j=2, u=2),
+            )
+            return grouped
+
+        def quantise(grouped, words, scales, first):
+            cols = slice(first, first + 2 * P)
+            nc.vector.quantize_mx(out=words[:, cols].bitcast(FP8X4), scales=scales[:, cols], in_=grouped[:])
+
+        def w_pair(first):
+            return w_raw[:].bitcast(F32)[:, first * WORDS // P : (first + 2 * P) * WORDS // P]
+
+        def x_pair(first_tile):
+            g, t = divmod(first_tile, RUN)
+            return x_raw[g][:].bitcast(F32)[:, t * WORDS : (t + 2) * WORDS]
+
+        def pack_w(part):
+            firsts = [part * FEATURES + pair * 2 * P for pair in range(PART_TILES // 2)]
+            grouped = [regroup(flip(w_pair(first))) for first in firsts]
+            for first, tile_pair in zip(firsts, grouped):
+                quantise(tile_pair, w_words, w_scales, first)
+
+        pack_w(Q)
+        head = [regroup(flip(x_pair(first_tile))) for first_tile in range(0, AHEAD, 2)]
+        for first_tile, tile_pair in zip(range(0, AHEAD, 2), head):
+            quantise(tile_pair, x_words, x_scales, first_tile * P)
+
+        def spread(first, width):
+            acc = psum.tile([P, FEATURES], F32, tag="acc1", bufs=banks["acc1"])
+            nc.tensor.matmul(acc[:, 0:width], lhsT=ones[:], rhs=rows[:, first : first + width], start=True, stop=True)
+            return acc
+
+        bias_all = {}
+        for part, first in ((Q, 0), (V, FEATURES)):
+            bias_all[part] = keep.tile([P, FEATURES], F32, name="bias_all%d" % part)
+            nc.vector.tensor_copy(out=bias_all[part][:], in_=spread(first, FEATURES)[:])
+        log_mul = keep.tile([P, HEADS], F32, name="log_mul")
+        nc.vector.tensor_scalar_min(out=log_mul[:], in0=spread(2 * FEATURES, 64)[:, 0:HEADS], scalar1=MAX_LOG_MUL)
+        nc.scalar.activation(out=shrink[:, 0:HEADS], in_=log_mul[:], func=ACT.Exp, scale=-2.0)
+
+        def tile_of(part, step):
+            index = step - part * LAG
+            return index if 0 <= index < N_TILES else None
+
+        acc = {}
+        staged = {}
+        q_squares = {}
+        norm2, shrunk, gain = {}, {}, {}
+
+        def by_head(ap):
+            return ap.rearrange("p (h d) -> p h d", h=HEADS)
+
+        def over_head(gain_cols):
+            return gain_cols.unsqueeze(2).to_broadcast([P, HEADS, HEAD_DIM])
+
+        def slot(part, step):
+            g, t = divmod(tile_of(part, step), RUN)
+            return staged[(part, g)][:, :, t, :]
+
+        def project(step):
+            for part in range(PARTS):
+                index = tile_of(part, step)
+                if index is None:
+                    continue
+                bank = psum.tile([P, FEATURES], F32, tag="acc%d" % part, bufs=banks["acc%d" % part])
+                nc.tensor.matmul_mx(
+                    out=bank[:],
+                    lhsT=x_words[:, index * P : (index + 1) * P].bitcast(FP8X4),
+                    lhsT_scale=x_scales[:, index * P : (index + 1) * P],
+                    rhs=w_words[:, part * FEATURES : (part + 1) * FEATURES].bitcast(FP8X4),
+                    rhs_scale=w_scales[:, part * FEATURES : (part + 1) * FEATURES],
+                    start=True,
+                    stop=True,
+                )
+                acc[(part, step)] = bank
+
+        def new_stage(part, step):
+            index = tile_of(part, step)
+            if index is not None and index % RUN == 0:
+                staged[(part, index // RUN)] = stage.tile(
+                    [P, HEADS, RUN, HEAD_DIM], F32, name="staged%d" % part, tag="staged%d" % part
+                )
+
+        def add_bias(part, step):
+            if tile_of(part, step) is None:
+                return
+            new_stage(part, step)
+            nc.vector.tensor_tensor(
+                out=slot(part, step), in0=by_head(acc[(part, step)][:]), in1=by_head(bias_all[part][:]), op=ALU.add
+            )
+
+        def k_norms(step):
+            if tile_of(K, step) is None:
+                return
+            unread = work.tile([P, FEATURES], BF16, tag="unread")
+            for h in range(HEADS):
+                cols = slice(h * HEAD_DIM, (h + 1) * HEAD_DIM)
+                nc.scalar.activation(
+                    out=unread[:, cols],
+                    in_=acc[(K, step)][:, cols],
+                    func=ACT.Square,
+                    accum_out=norm2[step][:, HEADS + h : HEADS + h + 1],
+                )
+
+        def square_q(step):
+            if tile_of(Q, step) is None:
+                return
+            q_squares[step] = work.tile([P, HEADS, HEAD_DIM], F32, name="q_squares", tag="q_squares")
+            nc.scalar.activation(out=q_squares[step][:], in_=slot(Q, step), func=ACT.Square)
+
+        def q_norms(step):
+            if tile_of(Q, step) is None:
+                return
+            nc.vector.tensor_reduce(out=norm2[step][:, 0:HEADS], in_=q_squares[step][:], axis=AXIS.X, op=ALU.add)
+
+        def live(step):
+            parts = [part for part in (Q, K) if tile_of(part, step) is not None]
+            return slice(parts[0] * HEADS, (parts[-1] + 1) * HEADS) if parts else None
+
+        def store(part, step):
+            index = tile_of(part, step)
+            if index is None or index % RUN != RUN - 1:
+                return
+            for j in range(GROUP_BATCHES):
+                nc.sync.dma_start(
+                    out=outs[part][(index // RUN) * GROUP_BATCHES + j].rearrange("h (c t) d -> c h (t d)", t=RUN),
+                    in_=staged[(part, index // RUN)][j:P:GROUP_BATCHES].rearrange("p h t d -> p h (t d)"),
+                )
+
+        project(0)
+        waiting = None
+        for step in range(N_STEPS):
+            before = step - 1
+            packs = step % 2 == 0 and step + AHEAD < N_TILES
+            if packs:
+                flipped = flip(x_pair(step + AHEAD))
+            project(step + 1)
+
+            if live(step) is not None:
+                norm2[step] = small.tile([P, 2 * HEADS], F32, name="norm2", tag="norm2")
+            add_bias(Q, step)
+            new_stage(K, step)
+            k_norms(step)
+            q_norms(before)
+            cols = live(before)
+            if cols is not None:
+                shrunk[before] = small.tile([P, 2 * HEADS], F32, name="shrunk", tag="shrunk")
+                nc.vector.scalar_tensor_tensor(
+                    out=shrunk[before][:, cols], in0=norm2[before][:, cols], scalar=EPS * EPS, in1=shrink[:, cols],
+                    op0=ALU.max, op1=ALU.mult,
+                )
+                gain[before] = small.tile([P, 2 * HEADS], F32, name="gain", tag="gain")
+                nc.scalar.activation(out=gain[before][:, cols], in_=shrunk[before][:, cols], func=ACT.Abs_reciprocal_sqrt)
+            square_q(step)
+            add_bias(V, step)
+            store(V, step)
+            if waiting is not None:
+                quantise(waiting[0], x_words, x_scales, waiting[1] * P)
+                waiting = None
+            if tile_of(K, before) is not None:
+                nc.vector.tensor_tensor(
+                    out=slot(K, before), in0=by_head(acc[(K, before)][:]),
+                    in1=over_head(gain[before][:, HEADS : 2 * HEADS]), op=ALU.mult,
+                )
+                store(K, before)
+            if tile_of(Q, before) is not None:
+                nc.gpsimd.tensor_tensor(
+                    out=slot(Q, before), in0=slot(Q, before), in1=over_head(gain[before][:, 0:HEADS]), op=ALU.mult
+                )
+                store(Q, before)
+            if packs:
+                waiting = (regroup(flipped), step + AHEAD)
+            for part in (K, V):
+                if step == (part - 1) * LAG:
+                    pack_w(part)

@@ -150,7 +150,8 @@ def tile_selfattention_pa_t_kernel(
 
         acc = {}
         staged = {}
-        q_squares = {}
+        stats = {}
+        mean_part = {}
         norm2, shrunk, gain = {}, {}, {}
 
         def by_head(ap):
@@ -208,16 +209,31 @@ def tile_selfattention_pa_t_kernel(
                     accum_out=norm2[step][:, HEADS + h : HEADS + h + 1],
                 )
 
-        def square_q(step):
+        def q_stats(step):
             if tile_of(Q, step) is None:
                 return
-            q_squares[step] = work.tile([P, HEADS, HEAD_DIM], F32, name="q_squares", tag="q_squares")
-            nc.scalar.activation(out=q_squares[step][:], in_=slot(Q, step), func=ACT.Square)
+            stats[step] = small.tile([P, HEADS, 3], F32, name="stats", tag="stats")
+            for h in range(0, HEADS, 2):
+                nc.vector.bn_stats(
+                    out=stats[step][:, h : h + 2, :].rearrange("p h s -> p (h s)"),
+                    in_=slot(Q, step)[:, h : h + 2, :].rearrange("p h d -> p d h"),
+                )
+
+        def q_mean_part(step):
+            if tile_of(Q, step) is None:
+                return
+            mean_part[step] = small.tile([P, HEADS], F32, name="mean_part", tag="mean_part")
+            nc.vector.scalar_tensor_tensor(
+                out=mean_part[step][:], in0=stats[step][:, :, 1], scalar=float(HEAD_DIM), in1=stats[step][:, :, 1],
+                op0=ALU.mult, op1=ALU.mult,
+            )
 
         def q_norms(step):
             if tile_of(Q, step) is None:
                 return
-            nc.vector.tensor_reduce(out=norm2[step][:, 0:HEADS], in_=q_squares[step][:], axis=AXIS.X, op=ALU.add)
+            nc.vector.tensor_tensor(
+                out=norm2[step][:, 0:HEADS], in0=mean_part[step][:], in1=stats[step][:, :, 2], op=ALU.add
+            )
 
         def live(step):
             parts = [part for part in (Q, K) if tile_of(part, step) is not None]
@@ -248,6 +264,8 @@ def tile_selfattention_pa_t_kernel(
             new_stage(K, step)
             k_norms(step)
             q_norms(before)
+            add_bias(V, step)
+            store(V, step)
             cols = live(before)
             if cols is not None:
                 shrunk[before] = small.tile([P, 2 * HEADS], F32, name="shrunk", tag="shrunk")
@@ -257,17 +275,19 @@ def tile_selfattention_pa_t_kernel(
                 )
                 gain[before] = small.tile([P, 2 * HEADS], F32, name="gain", tag="gain")
                 nc.scalar.activation(out=gain[before][:, cols], in_=shrunk[before][:, cols], func=ACT.Abs_reciprocal_sqrt)
-            square_q(step)
-            add_bias(V, step)
-            store(V, step)
+            q_stats(step)
             if waiting is not None:
                 quantise(waiting[0], x_words, x_scales, waiting[1] * P)
                 waiting = None
+            q_mean_part(step)
             if tile_of(K, before) is not None:
-                nc.vector.tensor_tensor(
-                    out=slot(K, before), in0=by_head(acc[(K, before)][:]),
-                    in1=over_head(gain[before][:, HEADS : 2 * HEADS]), op=ALU.mult,
-                )
+                for h in range(HEADS):
+                    nc.scalar.activation(
+                        out=slot(K, before)[:, h, :],
+                        in_=acc[(K, before)][:, h * HEAD_DIM : (h + 1) * HEAD_DIM],
+                        func=ACT.Copy,
+                        scale=gain[before][:, HEADS + h : HEADS + h + 1],
+                    )
                 store(K, before)
             if tile_of(Q, before) is not None:
                 nc.gpsimd.tensor_tensor(

@@ -22,13 +22,16 @@ Q, K, V = 0, 1, 2
 MAX_LOG_MUL = math.log(100.0)
 EPS = 1e-12
 
-GROUP_BATCHES = 2
-GROUPS = BATCHES // GROUP_BATCHES
-RUN = GROUP_BATCHES * TOKENS // P
-N_TILES = GROUPS * RUN
+GROUP_BATCHES = (1, 1, 2, 2, 1, 1)
+GROUPS = len(GROUP_BATCHES)
+RUNS = [batches * TOKENS // P for batches in GROUP_BATCHES]
+FIRST_BATCH = [sum(GROUP_BATCHES[:g]) for g in range(GROUPS)]
+PLACE = [(g, t) for g in range(GROUPS) for t in range(RUNS[g])]
+N_TILES = len(PLACE)
 PART_TILES = FEATURES // P
-AHEAD = 4
-LAG = 3
+AHEAD = 3
+V_HEADS = 5
+LAG = 2
 N_STEPS = N_TILES + (PARTS - 1) * LAG
 
 FLOPS = 2 * BATCHES * TOKENS * FEATURES * PARTS * FEATURES
@@ -49,44 +52,54 @@ def tile_selfattention_pa_t_kernel(
         banks = {"flipped": 2, "acc0": 2, "acc1": 3, "acc2": 1}
 
         w_raw = keep.tile([P, PARTS * PART_TILES * FEATURES], BF16, name="w_raw")
-        x_raw = [keep.tile([P, RUN * FEATURES], BF16, name="x_raw%d" % g) for g in range(GROUPS)]
+        x_raw = [keep.tile([P, RUNS[g] * FEATURES], BF16, name="x_raw%d" % g) for g in range(GROUPS)]
         rows = keep.tile([P, 2 * FEATURES + 64], BF16, name="rows")
-        nc.vector.memset(rows[:], 0.0)
-        nc.scalar.dma_start(out=rows[0:1, 0:FEATURES], in_=q_bias.rearrange("(o n) -> o n", o=1))
-        nc.scalar.dma_start(out=rows[0:1, FEATURES : 2 * FEATURES], in_=v_bias.rearrange("(o n) -> o n", o=1))
-        nc.scalar.dma_start(
-            out=rows[0:1, 2 * FEATURES : 2 * FEATURES + HEADS],
-            in_=log_scale_mul.rearrange("a h b c -> a (h b c)"),
-        )
 
-        def load_w(part):
-            nc.sync.dma_start(
-                out=w_raw[:, part * PART_TILES * FEATURES : (part + 1) * PART_TILES * FEATURES].rearrange(
-                    "p (n f) -> p n f", n=PART_TILES
-                ),
-                in_=w_qkv[part * FEATURES : (part + 1) * FEATURES, :].rearrange("(n p) f -> p n f", p=P),
-            )
-
-        def load_x(g):
-            for j in range(GROUP_BATCHES):
+        def load_w(part, halves=1):
+            tiles = PART_TILES // halves
+            for first in range(part * PART_TILES, (part + 1) * PART_TILES, tiles):
                 nc.sync.dma_start(
-                    out=x_raw[g][j:P:GROUP_BATCHES, :],
-                    in_=x[g * GROUP_BATCHES + j].rearrange("(c t) f -> c (t f)", t=RUN),
+                    out=w_raw[:, first * FEATURES : (first + tiles) * FEATURES].rearrange("p (n f) -> p n f", n=tiles),
+                    in_=w_qkv[first * P : (first + tiles) * P, :].rearrange("(n p) f -> p n f", p=P),
                 )
 
-        load_w(Q)
-        load_x(0)
-        load_w(K)
-        load_w(V)
-        for g in range(1, GROUPS):
-            load_x(g)
+        def load_x(g):
+            n = GROUP_BATCHES[g]
+            for j in range(n):
+                nc.sync.dma_start(
+                    out=x_raw[g][j:P:n, :],
+                    in_=x[FIRST_BATCH[g] + j].rearrange("(c t) f -> c (t f)", t=RUNS[g]),
+                )
+
+        def load_vectors():
+            nc.sync.dma_start(out=rows[0:1, 0:FEATURES], in_=q_bias.rearrange("(o n) -> o n", o=1))
+            nc.sync.dma_start(
+                out=rows[0:1, 2 * FEATURES : 2 * FEATURES + HEADS],
+                in_=log_scale_mul.rearrange("a h b c -> a (h b c)"),
+            )
+            nc.sync.dma_start(out=rows[0:1, FEATURES : 2 * FEATURES], in_=v_bias.rearrange("(o n) -> o n", o=1))
 
         ident = keep.tile([P, P], F32, name="ident")
         make_identity(nc, ident[:])
+        nc.gpsimd.memset(rows[:].bitcast(F32), 0.0)
+        table = keep.tile([P, 2], F32, name="table")
+        nc.vector.memset(table[:, 0:1], 1.0)
+        nc.scalar.activation(out=table[:, 1:2], in_=table[:, 0:1], func=ACT.Abs_reciprocal_sqrt)
         ones = keep.tile([P, P], BF16, name="ones")
         nc.vector.memset(ones[:], 1.0)
         shrink = keep.tile([P, 2 * HEADS], F32, name="shrink")
         nc.vector.memset(shrink[:, HEADS : 2 * HEADS], 1.0)
+        two = keep.tile([P, HEADS], F32, name="two")
+        nc.vector.memset(two[:], 2.0)
+
+        load_w(Q, halves=2)
+        load_x(0)
+        load_vectors()
+        load_w(K)
+        load_x(1)
+        load_w(V)
+        for g in range(2, GROUPS):
+            load_x(g)
 
         w_words = keep.tile([P, PARTS * FEATURES], U32, name="w_words", align_bytes=64)
         w_scales = keep.tile([P, PARTS * FEATURES], U8, name="w_scales", align_bytes=64)
@@ -101,9 +114,9 @@ def tile_selfattention_pa_t_kernel(
                 nc.tensor.transpose(flipped[:, cols], raw_words[:, j * WORDS + u : (j + 1) * WORDS : 2], ident[:])
             return flipped
 
-        def regroup(flipped):
+        def regroup(flipped, copy=nc.scalar.copy):
             grouped = work.tile([P, 8 * P], BF16, tag="grouped", align_bytes=64)
-            nc.scalar.copy(
+            copy(
                 out=grouped[:].bitcast(F32).rearrange("p (j r u) -> p j r u", j=2, u=2),
                 in_=flipped[:].rearrange("p (j u r) -> p j r u", j=2, u=2),
             )
@@ -117,32 +130,31 @@ def tile_selfattention_pa_t_kernel(
             return w_raw[:].bitcast(F32)[:, first * WORDS // P : (first + 2 * P) * WORDS // P]
 
         def x_pair(first_tile):
-            g, t = divmod(first_tile, RUN)
+            g, t = PLACE[first_tile]
             return x_raw[g][:].bitcast(F32)[:, t * WORDS : (t + 2) * WORDS]
 
-        def pack_w(part):
-            firsts = [part * FEATURES + pair * 2 * P for pair in range(PART_TILES // 2)]
-            grouped = [regroup(flip(w_pair(first))) for first in firsts]
-            for first, tile_pair in zip(firsts, grouped):
-                quantise(tile_pair, w_words, w_scales, first)
-
-        pack_w(Q)
-        head = [regroup(flip(x_pair(first_tile))) for first_tile in range(0, AHEAD, 2)]
-        for first_tile, tile_pair in zip(range(0, AHEAD, 2), head):
-            quantise(tile_pair, x_words, x_scales, first_tile * P)
+        w_pairs = {part: [part * FEATURES + pair * 2 * P for pair in range(PART_TILES // 2)] for part in (Q, K, V)}
+        flipped_w = [flip(w_pair(first)) for first in w_pairs[Q]]
+        grouped_w = [regroup(flipped_w[0]), regroup(flipped_w[1], nc.vector.tensor_copy)]
+        grouped_x = regroup(flip(x_pair(0)))
+        for first, tile_pair in zip(w_pairs[Q], grouped_w):
+            quantise(tile_pair, w_words, w_scales, first)
 
         def spread(first, width):
             acc = psum.tile([P, FEATURES], F32, tag="acc1", bufs=banks["acc1"])
             nc.tensor.matmul(acc[:, 0:width], lhsT=ones[:], rhs=rows[:, first : first + width], start=True, stop=True)
             return acc
 
-        bias_all = {}
-        for part, first in ((Q, 0), (V, FEATURES)):
-            bias_all[part] = keep.tile([P, FEATURES], F32, name="bias_all%d" % part)
-            nc.vector.tensor_copy(out=bias_all[part][:], in_=spread(first, FEATURES)[:])
-        log_mul = keep.tile([P, HEADS], F32, name="log_mul")
-        nc.vector.tensor_scalar_min(out=log_mul[:], in0=spread(2 * FEATURES, 64)[:, 0:HEADS], scalar1=MAX_LOG_MUL)
-        nc.scalar.activation(out=shrink[:, 0:HEADS], in_=log_mul[:], func=ACT.Exp, scale=-2.0)
+        bias_all = {part: keep.tile([P, FEATURES], F32, name="bias_all%d" % part) for part in (Q, V)}
+        nc.scalar.copy(out=bias_all[Q][:], in_=spread(0, FEATURES)[:])
+        exponent = keep.tile([P, HEADS], F32, name="exponent")
+        nc.vector.tensor_scalar(
+            out=exponent[:], in0=spread(2 * FEATURES, 64)[:, 0:HEADS], scalar1=MAX_LOG_MUL,
+            scalar2=-2.0 / math.log(2.0), op0=ALU.min, op1=ALU.mult,
+        )
+        nc.gpsimd.tensor_tensor(out=shrink[:, 0:HEADS], in0=two[:], in1=exponent[:], op=ALU.pow)
+        quantise(grouped_x, x_words, x_scales, 0)
+        nc.scalar.copy(out=bias_all[V][:], in_=spread(FEATURES, FEATURES)[:])
 
         def tile_of(part, step):
             index = step - part * LAG
@@ -157,11 +169,8 @@ def tile_selfattention_pa_t_kernel(
         def by_head(ap):
             return ap.rearrange("p (h d) -> p h d", h=HEADS)
 
-        def over_head(gain_cols):
-            return gain_cols.unsqueeze(2).to_broadcast([P, HEADS, HEAD_DIM])
-
         def slot(part, step):
-            g, t = divmod(tile_of(part, step), RUN)
+            g, t = PLACE[tile_of(part, step)]
             return staged[(part, g)][:, :, t, :]
 
         def project(step):
@@ -183,9 +192,10 @@ def tile_selfattention_pa_t_kernel(
 
         def new_stage(part, step):
             index = tile_of(part, step)
-            if index is not None and index % RUN == 0:
-                staged[(part, index // RUN)] = stage.tile(
-                    [P, HEADS, RUN, HEAD_DIM], F32, name="staged%d" % part, tag="staged%d" % part
+            if index is not None and PLACE[index][1] == 0:
+                g = PLACE[index][0]
+                staged[(part, g)] = stage.tile(
+                    [P, HEADS, RUNS[g], HEAD_DIM], F32, name="staged%d" % part, tag="staged%d_%d" % (part, RUNS[g])
                 )
 
         def add_bias(part, step):
@@ -241,22 +251,29 @@ def tile_selfattention_pa_t_kernel(
 
         def store(part, step):
             index = tile_of(part, step)
-            if index is None or index % RUN != RUN - 1:
+            if index is None:
                 return
-            for j in range(GROUP_BATCHES):
+            g, t = PLACE[index]
+            if t != RUNS[g] - 1:
+                return
+            n = GROUP_BATCHES[g]
+            for j in range(n):
                 nc.sync.dma_start(
-                    out=outs[part][(index // RUN) * GROUP_BATCHES + j].rearrange("h (c t) d -> c h (t d)", t=RUN),
-                    in_=staged[(part, index // RUN)][j:P:GROUP_BATCHES].rearrange("p h t d -> p h (t d)"),
+                    out=outs[part][FIRST_BATCH[g] + j].rearrange("h (c t) d -> c h (t d)", t=RUNS[g]),
+                    in_=staged[(part, g)][j:P:n].rearrange("p h t d -> p h (t d)"),
                 )
 
         project(0)
-        waiting = None
+        waiting = [(regroup(flip(x_pair(2))), x_words, x_scales, 2 * P)]
         for step in range(N_STEPS):
             before = step - 1
-            packs = step % 2 == 0 and step + AHEAD < N_TILES
-            if packs:
-                flipped = flip(x_pair(step + AHEAD))
-            project(step + 1)
+            flips = []
+            if step % 2 == 1 and step + AHEAD < N_TILES:
+                first_tile = step + AHEAD
+                flips = [(flip(x_pair(first_tile)), x_words, x_scales, first_tile * P)]
+            for part in (K, V):
+                if step == (part - 1) * LAG:
+                    flips = [(flip(w_pair(first)), w_words, w_scales, first) for first in w_pairs[part]]
 
             if live(step) is not None:
                 norm2[step] = small.tile([P, 2 * HEADS], F32, name="norm2", tag="norm2")
@@ -276,10 +293,10 @@ def tile_selfattention_pa_t_kernel(
                 gain[before] = small.tile([P, 2 * HEADS], F32, name="gain", tag="gain")
                 nc.scalar.activation(out=gain[before][:, cols], in_=shrunk[before][:, cols], func=ACT.Abs_reciprocal_sqrt)
             q_stats(step)
-            if waiting is not None:
-                quantise(waiting[0], x_words, x_scales, waiting[1] * P)
-                waiting = None
+            for tile_pair, words, scales, first in waiting:
+                quantise(tile_pair, words, scales, first)
             q_mean_part(step)
+            project(step + 1)
             if tile_of(K, before) is not None:
                 for h in range(HEADS):
                     nc.scalar.activation(
@@ -290,12 +307,11 @@ def tile_selfattention_pa_t_kernel(
                     )
                 store(K, before)
             if tile_of(Q, before) is not None:
-                nc.gpsimd.tensor_tensor(
-                    out=slot(Q, before), in0=slot(Q, before), in1=over_head(gain[before][:, 0:HEADS]), op=ALU.mult
-                )
+                for h in range(HEADS):
+                    cols, factor = slot(Q, before)[:, h, :], gain[before][:, h : h + 1]
+                    if h < V_HEADS:
+                        nc.vector.tensor_scalar_mul(out=cols, in0=cols, scalar1=factor)
+                    else:
+                        nc.scalar.activation(out=cols, in_=cols, func=ACT.Copy, scale=factor)
                 store(Q, before)
-            if packs:
-                waiting = (regroup(flipped), step + AHEAD)
-            for part in (K, V):
-                if step == (part - 1) * LAG:
-                    pack_w(part)
+            waiting = [(regroup(bank), words, scales, first) for bank, words, scales, first in flips]

@@ -87,8 +87,10 @@ def tile_selfattention_pa_t_kernel(
         nc.scalar.activation(out=table[:, 1:2], in_=table[:, 0:1], func=ACT.Abs_reciprocal_sqrt)
         ones = keep.tile([P, P], BF16, name="ones")
         nc.vector.memset(ones[:], 1.0)
-        shrink = keep.tile([P, 2 * HEADS], F32, name="shrink")
-        nc.vector.memset(shrink[:, HEADS : 2 * HEADS], 1.0)
+        shrink = keep.tile([P, HEADS], F32, name="shrink")
+        floor = keep.tile([P, 2], F32, name="floor")
+        nc.vector.memset(floor[:, 0:1], -EPS * EPS)
+        nc.vector.memset(floor[:, 1:2], EPS * EPS)
         two = keep.tile([P, HEADS], F32, name="two")
         nc.vector.memset(two[:], 2.0)
 
@@ -152,7 +154,7 @@ def tile_selfattention_pa_t_kernel(
             out=exponent[:], in0=spread(2 * FEATURES, 64)[:, 0:HEADS], scalar1=MAX_LOG_MUL,
             scalar2=-2.0 / math.log(2.0), op0=ALU.min, op1=ALU.mult,
         )
-        nc.gpsimd.tensor_tensor(out=shrink[:, 0:HEADS], in0=two[:], in1=exponent[:], op=ALU.pow)
+        nc.gpsimd.tensor_tensor(out=shrink[:], in0=two[:], in1=exponent[:], op=ALU.pow)
         quantise(grouped_x, x_words, x_scales, 0)
         nc.scalar.copy(out=bias_all[V][:], in_=spread(FEATURES, FEATURES)[:])
 
@@ -163,8 +165,8 @@ def tile_selfattention_pa_t_kernel(
         acc = {}
         staged = {}
         stats = {}
-        mean_part = {}
-        norm2, shrunk, gain = {}, {}, {}
+        mean_part, norm2_q, shrunk, above = {}, {}, {}, {}
+        norm2_k, gain_q, gain_k = {}, {}, {}
 
         def by_head(ap):
             return ap.rearrange("p (h d) -> p h d", h=HEADS)
@@ -209,6 +211,7 @@ def tile_selfattention_pa_t_kernel(
         def k_norms(step):
             if tile_of(K, step) is None:
                 return
+            norm2_k[step] = small.tile([P, HEADS], F32, name="norm2_k", tag="norm2_k")
             unread = work.tile([P, FEATURES], BF16, tag="unread")
             for h in range(HEADS):
                 cols = slice(h * HEAD_DIM, (h + 1) * HEAD_DIM)
@@ -216,7 +219,7 @@ def tile_selfattention_pa_t_kernel(
                     out=unread[:, cols],
                     in_=acc[(K, step)][:, cols],
                     func=ACT.Square,
-                    accum_out=norm2[step][:, HEADS + h : HEADS + h + 1],
+                    accum_out=norm2_k[step][:, h : h + 1],
                 )
 
         def q_stats(step):
@@ -241,13 +244,57 @@ def tile_selfattention_pa_t_kernel(
         def q_norms(step):
             if tile_of(Q, step) is None:
                 return
-            nc.vector.tensor_tensor(
-                out=norm2[step][:, 0:HEADS], in0=mean_part[step][:], in1=stats[step][:, :, 2], op=ALU.add
+            norm2_q[step] = small.tile([P, HEADS], F32, name="norm2_q", tag="norm2_q")
+            nc.vector.tensor_tensor(out=norm2_q[step][:], in0=mean_part[step][:], in1=stats[step][:, :, 2], op=ALU.add)
+
+        def q_shrink(step):
+            if tile_of(Q, step) is None:
+                return
+            shrunk[step] = small.tile([P, HEADS], F32, name="shrunk", tag="shrunk")
+            nc.vector.scalar_tensor_tensor(
+                out=shrunk[step][:], in0=norm2_q[step][:], scalar=EPS * EPS, in1=shrink[:], op0=ALU.max, op1=ALU.mult
             )
 
-        def live(step):
-            parts = [part for part in (Q, K) if tile_of(part, step) is not None]
-            return slice(parts[0] * HEADS, (parts[-1] + 1) * HEADS) if parts else None
+        def q_gains(step):
+            if tile_of(Q, step) is None:
+                return
+            gain_q[step] = small.tile([P, HEADS], F32, name="gain_q", tag="gain_q")
+            nc.scalar.activation(out=gain_q[step][:], in_=shrunk[step][:], func=ACT.Abs_reciprocal_sqrt)
+
+        def q_scale(step, heads, on_vector):
+            if tile_of(Q, step) is None:
+                return
+            for h in heads:
+                cols, factor = slot(Q, step)[:, h, :], gain_q[step][:, h : h + 1]
+                if on_vector:
+                    nc.vector.tensor_scalar_mul(out=cols, in0=cols, scalar1=factor)
+                else:
+                    nc.scalar.activation(out=cols, in_=cols, func=ACT.Copy, scale=factor)
+
+        def k_relu(step):
+            if tile_of(K, step) is None:
+                return
+            above[step] = small.tile([P, HEADS], F32, name="above", tag="above")
+            nc.scalar.activation(out=above[step][:], in_=norm2_k[step][:], func=ACT.Relu, bias=floor[:, 0:1])
+
+        def k_gains(step):
+            if tile_of(K, step) is None:
+                return
+            gain_k[step] = small.tile([P, HEADS], F32, name="gain_k", tag="gain_k")
+            nc.scalar.activation(
+                out=gain_k[step][:], in_=above[step][:], func=ACT.Abs_reciprocal_sqrt, bias=floor[:, 1:2]
+            )
+
+        def k_scale(step):
+            if tile_of(K, step) is None:
+                return
+            for h in range(HEADS):
+                nc.scalar.activation(
+                    out=slot(K, step)[:, h, :],
+                    in_=acc[(K, step)][:, h * HEAD_DIM : (h + 1) * HEAD_DIM],
+                    func=ACT.Copy,
+                    scale=gain_k[step][:, h : h + 1],
+                )
 
         def store(part, step):
             index = tile_of(part, step)
@@ -266,7 +313,6 @@ def tile_selfattention_pa_t_kernel(
         project(0)
         waiting = [(regroup(flip(x_pair(2))), x_words, x_scales, 2 * P)]
         for step in range(N_STEPS):
-            before = step - 1
             flips = []
             if step % 2 == 1 and step + AHEAD < N_TILES:
                 first_tile = step + AHEAD
@@ -275,43 +321,24 @@ def tile_selfattention_pa_t_kernel(
                 if step == (part - 1) * LAG:
                     flips = [(flip(w_pair(first)), w_words, w_scales, first) for first in w_pairs[part]]
 
-            if live(step) is not None:
-                norm2[step] = small.tile([P, 2 * HEADS], F32, name="norm2", tag="norm2")
             add_bias(Q, step)
             new_stage(K, step)
             k_norms(step)
-            q_norms(before)
+            q_norms(step - 1)
             add_bias(V, step)
             store(V, step)
-            cols = live(before)
-            if cols is not None:
-                shrunk[before] = small.tile([P, 2 * HEADS], F32, name="shrunk", tag="shrunk")
-                nc.vector.scalar_tensor_tensor(
-                    out=shrunk[before][:, cols], in0=norm2[before][:, cols], scalar=EPS * EPS, in1=shrink[:, cols],
-                    op0=ALU.max, op1=ALU.mult,
-                )
-                gain[before] = small.tile([P, 2 * HEADS], F32, name="gain", tag="gain")
-                nc.scalar.activation(out=gain[before][:, cols], in_=shrunk[before][:, cols], func=ACT.Abs_reciprocal_sqrt)
+            q_shrink(step - 1)
             q_stats(step)
             for tile_pair, words, scales, first in waiting:
                 quantise(tile_pair, words, scales, first)
             q_mean_part(step)
             project(step + 1)
-            if tile_of(K, before) is not None:
-                for h in range(HEADS):
-                    nc.scalar.activation(
-                        out=slot(K, before)[:, h, :],
-                        in_=acc[(K, before)][:, h * HEAD_DIM : (h + 1) * HEAD_DIM],
-                        func=ACT.Copy,
-                        scale=gain[before][:, HEADS + h : HEADS + h + 1],
-                    )
-                store(K, before)
-            if tile_of(Q, before) is not None:
-                for h in range(HEADS):
-                    cols, factor = slot(Q, before)[:, h, :], gain[before][:, h : h + 1]
-                    if h < V_HEADS:
-                        nc.vector.tensor_scalar_mul(out=cols, in0=cols, scalar1=factor)
-                    else:
-                        nc.scalar.activation(out=cols, in_=cols, func=ACT.Copy, scale=factor)
-                store(Q, before)
             waiting = [(regroup(bank), words, scales, first) for bank, words, scales, first in flips]
+            q_scale(step - 2, range(V_HEADS), True)
+            q_scale(step - 2, range(V_HEADS, HEADS), False)
+            store(Q, step - 2)
+            k_relu(step)
+            k_scale(step - 1)
+            store(K, step - 1)
+            k_gains(step)
+            q_gains(step - 1)

@@ -30,7 +30,6 @@ PLACE = [(g, t) for g in range(GROUPS) for t in range(RUNS[g])]
 N_TILES = len(PLACE)
 PART_TILES = FEATURES // P
 AHEAD = 3
-V_HEADS = 5
 LAG = 2
 N_STEPS = N_TILES + (PARTS - 1) * LAG
 
@@ -164,9 +163,8 @@ def tile_selfattention_pa_t_kernel(
 
         acc = {}
         staged = {}
-        stats = {}
-        mean_part, norm2_q, shrunk, above = {}, {}, {}, {}
-        norm2_k, gain_q, gain_k = {}, {}, {}
+        norm2, gain = {}, {}
+        shrunk, above = {}, {}
 
         def by_head(ap):
             return ap.rearrange("p (h d) -> p h d", h=HEADS)
@@ -208,93 +206,63 @@ def tile_selfattention_pa_t_kernel(
                 out=slot(part, step), in0=by_head(acc[(part, step)][:]), in1=by_head(bias_all[part][:]), op=ALU.add
             )
 
-        def k_norms(step):
-            if tile_of(K, step) is None:
+        def norms(part, step):
+            if tile_of(part, step) is None:
                 return
-            norm2_k[step] = small.tile([P, HEADS], F32, name="norm2_k", tag="norm2_k")
+            norm2[(part, step)] = small.tile([P, HEADS], F32, name="norm2_%d" % part, tag="norm2_%d" % part)
             unread = work.tile([P, FEATURES], BF16, tag="unread")
             for h in range(HEADS):
                 cols = slice(h * HEAD_DIM, (h + 1) * HEAD_DIM)
                 nc.scalar.activation(
                     out=unread[:, cols],
-                    in_=acc[(K, step)][:, cols],
+                    in_=acc[(K, step)][:, cols] if part == K else slot(Q, step)[:, h, :],
                     func=ACT.Square,
-                    accum_out=norm2_k[step][:, h : h + 1],
+                    accum_out=norm2[(part, step)][:, h : h + 1],
                 )
-
-        def q_stats(step):
-            if tile_of(Q, step) is None:
-                return
-            stats[step] = small.tile([P, HEADS, 3], F32, name="stats", tag="stats")
-            for h in range(0, HEADS, 2):
-                nc.vector.bn_stats(
-                    out=stats[step][:, h : h + 2, :].rearrange("p h s -> p (h s)"),
-                    in_=slot(Q, step)[:, h : h + 2, :].rearrange("p h d -> p d h"),
-                )
-
-        def q_mean_part(step):
-            if tile_of(Q, step) is None:
-                return
-            mean_part[step] = small.tile([P, HEADS], F32, name="mean_part", tag="mean_part")
-            nc.vector.scalar_tensor_tensor(
-                out=mean_part[step][:], in0=stats[step][:, :, 1], scalar=float(HEAD_DIM), in1=stats[step][:, :, 1],
-                op0=ALU.mult, op1=ALU.mult,
-            )
-
-        def q_norms(step):
-            if tile_of(Q, step) is None:
-                return
-            norm2_q[step] = small.tile([P, HEADS], F32, name="norm2_q", tag="norm2_q")
-            nc.vector.tensor_tensor(out=norm2_q[step][:], in0=mean_part[step][:], in1=stats[step][:, :, 2], op=ALU.add)
 
         def q_shrink(step):
             if tile_of(Q, step) is None:
                 return
             shrunk[step] = small.tile([P, HEADS], F32, name="shrunk", tag="shrunk")
             nc.vector.scalar_tensor_tensor(
-                out=shrunk[step][:], in0=norm2_q[step][:], scalar=EPS * EPS, in1=shrink[:], op0=ALU.max, op1=ALU.mult
+                out=shrunk[step][:], in0=norm2[(Q, step)][:], scalar=EPS * EPS, in1=shrink[:], op0=ALU.max, op1=ALU.mult
             )
 
         def q_gains(step):
             if tile_of(Q, step) is None:
                 return
-            gain_q[step] = small.tile([P, HEADS], F32, name="gain_q", tag="gain_q")
-            nc.scalar.activation(out=gain_q[step][:], in_=shrunk[step][:], func=ACT.Abs_reciprocal_sqrt)
+            gain[(Q, step)] = small.tile([P, HEADS], F32, name="gain_q", tag="gain_q")
+            nc.scalar.activation(out=gain[(Q, step)][:], in_=shrunk[step][:], func=ACT.Abs_reciprocal_sqrt)
 
-        def q_scale(step, heads, on_vector):
+        def q_scale(step):
             if tile_of(Q, step) is None:
                 return
-            for h in heads:
-                cols, factor = slot(Q, step)[:, h, :], gain_q[step][:, h : h + 1]
-                if on_vector:
-                    nc.vector.tensor_scalar_mul(out=cols, in0=cols, scalar1=factor)
-                else:
-                    nc.scalar.activation(out=cols, in_=cols, func=ACT.Copy, scale=factor)
+            for h in range(HEADS):
+                cols = slot(Q, step)[:, h, :]
+                nc.vector.tensor_scalar_mul(out=cols, in0=cols, scalar1=gain[(Q, step)][:, h : h + 1])
 
         def k_relu(step):
             if tile_of(K, step) is None:
                 return
             above[step] = small.tile([P, HEADS], F32, name="above", tag="above")
-            nc.scalar.activation(out=above[step][:], in_=norm2_k[step][:], func=ACT.Relu, bias=floor[:, 0:1])
+            nc.scalar.activation(out=above[step][:], in_=norm2[(K, step)][:], func=ACT.Relu, bias=floor[:, 0:1])
 
         def k_gains(step):
             if tile_of(K, step) is None:
                 return
-            gain_k[step] = small.tile([P, HEADS], F32, name="gain_k", tag="gain_k")
+            gain[(K, step)] = small.tile([P, HEADS], F32, name="gain_k", tag="gain_k")
             nc.scalar.activation(
-                out=gain_k[step][:], in_=above[step][:], func=ACT.Abs_reciprocal_sqrt, bias=floor[:, 1:2]
+                out=gain[(K, step)][:], in_=above[step][:], func=ACT.Abs_reciprocal_sqrt, bias=floor[:, 1:2]
             )
 
         def k_scale(step):
             if tile_of(K, step) is None:
                 return
-            for h in range(HEADS):
-                nc.scalar.activation(
-                    out=slot(K, step)[:, h, :],
-                    in_=acc[(K, step)][:, h * HEAD_DIM : (h + 1) * HEAD_DIM],
-                    func=ACT.Copy,
-                    scale=gain_k[step][:, h : h + 1],
-                )
+            new_stage(K, step)
+            nc.vector.tensor_tensor(
+                out=slot(K, step), in0=by_head(acc[(K, step)][:]),
+                in1=gain[(K, step)][:].unsqueeze(2).to_broadcast([P, HEADS, HEAD_DIM]), op=ALU.mult,
+            )
 
         def store(part, step):
             index = tile_of(part, step)
@@ -322,23 +290,19 @@ def tile_selfattention_pa_t_kernel(
                     flips = [(flip(w_pair(first)), w_words, w_scales, first) for first in w_pairs[part]]
 
             add_bias(Q, step)
-            new_stage(K, step)
-            k_norms(step)
-            q_norms(step - 1)
+            norms(K, step)
             add_bias(V, step)
             store(V, step)
-            q_shrink(step - 1)
-            q_stats(step)
-            for tile_pair, words, scales, first in waiting:
-                quantise(tile_pair, words, scales, first)
-            q_mean_part(step)
-            project(step + 1)
-            waiting = [(regroup(bank), words, scales, first) for bank, words, scales, first in flips]
-            q_scale(step - 2, range(V_HEADS), True)
-            q_scale(step - 2, range(V_HEADS, HEADS), False)
-            store(Q, step - 2)
-            k_relu(step)
             k_scale(step - 1)
             store(K, step - 1)
+            q_shrink(step - 1)
+            for tile_pair, words, scales, first in waiting:
+                quantise(tile_pair, words, scales, first)
+            project(step + 1)
+            waiting = [(regroup(bank), words, scales, first) for bank, words, scales, first in flips]
+            k_relu(step)
+            norms(Q, step)
+            q_scale(step - 2)
+            store(Q, step - 2)
             k_gains(step)
             q_gains(step - 1)

@@ -22,16 +22,13 @@ Q, K, V = 0, 1, 2
 MAX_LOG_MUL = math.log(100.0)
 EPS = 1e-12
 
-GROUP_BATCHES = (1, 1, 2, 2, 1, 1)
-GROUPS = len(GROUP_BATCHES)
-RUNS = [batches * TOKENS // P for batches in GROUP_BATCHES]
-FIRST_BATCH = [sum(GROUP_BATCHES[:g]) for g in range(GROUPS)]
-PLACE = [(g, t) for g in range(GROUPS) for t in range(RUNS[g])]
-N_TILES = len(PLACE)
+RUN = TOKENS // P
+N_TILES = BATCHES * RUN
 PART_TILES = FEATURES // P
 AHEAD = 3
-LAG = 2
-N_STEPS = N_TILES + (PARTS - 1) * LAG
+WIDE = 5
+LAG = {Q: 0, K: 1, V: 4}
+N_STEPS = N_TILES + LAG[V]
 
 FLOPS = 2 * BATCHES * TOKENS * FEATURES * PARTS * FEATURES
 
@@ -46,12 +43,12 @@ def tile_selfattention_pa_t_kernel(
         keep = ctx.enter_context(tc.tile_pool(name="keep", bufs=1))
         work = ctx.enter_context(tc.tile_pool(name="work", bufs=3))
         small = ctx.enter_context(tc.tile_pool(name="small", bufs=4))
-        stage = ctx.enter_context(tc.tile_pool(name="stage", bufs=2))
+        stage = ctx.enter_context(tc.tile_pool(name="stage", bufs=3))
         psum = ctx.enter_context(tc.psum_pool(name="psum", bufs=1))
         banks = {"flipped": 2, "acc0": 2, "acc1": 3, "acc2": 1}
 
         w_raw = keep.tile([P, PARTS * PART_TILES * FEATURES], BF16, name="w_raw")
-        x_raw = [keep.tile([P, RUNS[g] * FEATURES], BF16, name="x_raw%d" % g) for g in range(GROUPS)]
+        x_raw = [keep.tile([P, RUN * FEATURES], BF16, name="x_raw%d" % b) for b in range(BATCHES)]
         rows = keep.tile([P, 2 * FEATURES + 64], BF16, name="rows")
 
         def load_w(part, halves=1):
@@ -62,12 +59,12 @@ def tile_selfattention_pa_t_kernel(
                     in_=w_qkv[first * P : (first + tiles) * P, :].rearrange("(n p) f -> p n f", p=P),
                 )
 
-        def load_x(g):
-            n = GROUP_BATCHES[g]
-            for j in range(n):
+        def load_x(batch, pieces=1):
+            width = RUN * FEATURES // pieces
+            for piece in range(pieces):
+                cols = slice(piece * width, (piece + 1) * width)
                 nc.sync.dma_start(
-                    out=x_raw[g][j:P:n, :],
-                    in_=x[FIRST_BATCH[g] + j].rearrange("(c t) f -> c (t f)", t=RUNS[g]),
+                    out=x_raw[batch][:, cols], in_=x[batch].rearrange("(c t) f -> c (t f)", t=RUN)[:, cols]
                 )
 
         def load_vectors():
@@ -94,13 +91,13 @@ def tile_selfattention_pa_t_kernel(
         nc.vector.memset(two[:], 2.0)
 
         load_w(Q, halves=2)
-        load_x(0)
+        load_x(0, pieces=2)
         load_vectors()
         load_w(K)
         load_x(1)
         load_w(V)
-        for g in range(2, GROUPS):
-            load_x(g)
+        for batch in range(2, BATCHES):
+            load_x(batch)
 
         w_words = keep.tile([P, PARTS * FEATURES], U32, name="w_words", align_bytes=64)
         w_scales = keep.tile([P, PARTS * FEATURES], U8, name="w_scales", align_bytes=64)
@@ -131,8 +128,8 @@ def tile_selfattention_pa_t_kernel(
             return w_raw[:].bitcast(F32)[:, first * WORDS // P : (first + 2 * P) * WORDS // P]
 
         def x_pair(first_tile):
-            g, t = PLACE[first_tile]
-            return x_raw[g][:].bitcast(F32)[:, t * WORDS : (t + 2) * WORDS]
+            batch, t = divmod(first_tile, RUN)
+            return x_raw[batch][:].bitcast(F32)[:, t * WORDS : (t + 2) * WORDS]
 
         w_pairs = {part: [part * FEATURES + pair * 2 * P for pair in range(PART_TILES // 2)] for part in (Q, K, V)}
         flipped_w = [flip(w_pair(first)) for first in w_pairs[Q]]
@@ -147,34 +144,27 @@ def tile_selfattention_pa_t_kernel(
             return acc
 
         bias_all = {part: keep.tile([P, FEATURES], F32, name="bias_all%d" % part) for part in (Q, V)}
-        nc.scalar.copy(out=bias_all[Q][:], in_=spread(0, FEATURES)[:])
-        exponent = keep.tile([P, HEADS], F32, name="exponent")
-        nc.vector.tensor_scalar(
-            out=exponent[:], in0=spread(2 * FEATURES, 64)[:, 0:HEADS], scalar1=MAX_LOG_MUL,
-            scalar2=-2.0 / math.log(2.0), op0=ALU.min, op1=ALU.mult,
-        )
-        nc.gpsimd.tensor_tensor(out=shrink[:], in0=two[:], in1=exponent[:], op=ALU.pow)
         quantise(grouped_x, x_words, x_scales, 0)
-        nc.scalar.copy(out=bias_all[V][:], in_=spread(FEATURES, FEATURES)[:])
+        nc.scalar.copy(out=bias_all[Q][:], in_=spread(0, FEATURES)[:])
 
         def tile_of(part, step):
-            index = step - part * LAG
+            index = step - LAG[part]
             return index if 0 <= index < N_TILES else None
 
         acc = {}
         staged = {}
         norm2, gain = {}, {}
-        shrunk, above = {}, {}
+        squares, shrunk, above = {}, {}, {}
 
         def by_head(ap):
             return ap.rearrange("p (h d) -> p h d", h=HEADS)
 
         def slot(part, step):
-            g, t = PLACE[tile_of(part, step)]
-            return staged[(part, g)][:, :, t, :]
+            batch, t = divmod(tile_of(part, step), RUN)
+            return staged[(part, batch)][:, :, t, :]
 
         def project(step):
-            for part in range(PARTS):
+            for part in (Q, K, V):
                 index = tile_of(part, step)
                 if index is None:
                     continue
@@ -192,10 +182,9 @@ def tile_selfattention_pa_t_kernel(
 
         def new_stage(part, step):
             index = tile_of(part, step)
-            if index is not None and PLACE[index][1] == 0:
-                g = PLACE[index][0]
-                staged[(part, g)] = stage.tile(
-                    [P, HEADS, RUNS[g], HEAD_DIM], F32, name="staged%d" % part, tag="staged%d_%d" % (part, RUNS[g])
+            if index is not None and index % RUN == 0:
+                staged[(part, index // RUN)] = stage.tile(
+                    [P, HEADS, RUN, HEAD_DIM], F32, name="staged%d" % part, tag="staged%d" % part
                 )
 
         def add_bias(part, step):
@@ -206,19 +195,31 @@ def tile_selfattention_pa_t_kernel(
                 out=slot(part, step), in0=by_head(acc[(part, step)][:]), in1=by_head(bias_all[part][:]), op=ALU.add
             )
 
-        def norms(part, step):
-            if tile_of(part, step) is None:
+        def accumulate(norm2_cols, squared):
+            unread = work.tile([P, HEAD_DIM], BF16, tag="unread", bufs=8)
+            nc.scalar.activation(out=unread[:], in_=squared, func=ACT.Square, accum_out=norm2_cols)
+
+        def k_norms(step, heads):
+            if tile_of(K, step) is None:
                 return
-            norm2[(part, step)] = small.tile([P, HEADS], F32, name="norm2_%d" % part, tag="norm2_%d" % part)
-            unread = work.tile([P, FEATURES], BF16, tag="unread")
-            for h in range(HEADS):
-                cols = slice(h * HEAD_DIM, (h + 1) * HEAD_DIM)
-                nc.scalar.activation(
-                    out=unread[:, cols],
-                    in_=acc[(K, step)][:, cols] if part == K else slot(Q, step)[:, h, :],
-                    func=ACT.Square,
-                    accum_out=norm2[(part, step)][:, h : h + 1],
-                )
+            if heads[0] == 0:
+                norm2[(K, step)] = small.tile([P, HEADS], F32, name="norm2_k", tag="norm2_k")
+            for h in heads:
+                accumulate(norm2[(K, step)][:, h : h + 1], acc[(K, step)][:, h * HEAD_DIM : (h + 1) * HEAD_DIM])
+
+        def q_norms(step):
+            if tile_of(Q, step) is None:
+                return
+            norm2[(Q, step)] = small.tile([P, HEADS], F32, name="norm2_q", tag="norm2_q")
+            squares[step] = work.tile([P, WIDE, HEAD_DIM], F32, name="squares", tag="squares", bufs=2)
+            nc.scalar.activation(out=squares[step][:], in_=slot(Q, step)[:, 0:WIDE, :], func=ACT.Square)
+            for h in range(WIDE, HEADS):
+                accumulate(norm2[(Q, step)][:, h : h + 1], slot(Q, step)[:, h, :])
+
+        def q_reduce(step):
+            if tile_of(Q, step) is None:
+                return
+            nc.vector.tensor_reduce(out=norm2[(Q, step)][:, 0:WIDE], in_=squares[step][:], axis=AXIS.X, op=ALU.add)
 
         def q_shrink(step):
             if tile_of(Q, step) is None:
@@ -234,12 +235,15 @@ def tile_selfattention_pa_t_kernel(
             gain[(Q, step)] = small.tile([P, HEADS], F32, name="gain_q", tag="gain_q")
             nc.scalar.activation(out=gain[(Q, step)][:], in_=shrunk[step][:], func=ACT.Abs_reciprocal_sqrt)
 
+        def over_head(gain_cols):
+            return gain_cols.unsqueeze(2).to_broadcast([P, HEADS, HEAD_DIM])
+
         def q_scale(step):
             if tile_of(Q, step) is None:
                 return
-            for h in range(HEADS):
-                cols = slot(Q, step)[:, h, :]
-                nc.vector.tensor_scalar_mul(out=cols, in0=cols, scalar1=gain[(Q, step)][:, h : h + 1])
+            nc.gpsimd.tensor_tensor(
+                out=slot(Q, step), in0=slot(Q, step), in1=over_head(gain[(Q, step)][:]), op=ALU.mult
+            )
 
         def k_relu(step):
             if tile_of(K, step) is None:
@@ -261,48 +265,57 @@ def tile_selfattention_pa_t_kernel(
             new_stage(K, step)
             nc.vector.tensor_tensor(
                 out=slot(K, step), in0=by_head(acc[(K, step)][:]),
-                in1=gain[(K, step)][:].unsqueeze(2).to_broadcast([P, HEADS, HEAD_DIM]), op=ALU.mult,
+                in1=over_head(gain[(K, step)][:]), op=ALU.mult,
             )
 
         def store(part, step):
             index = tile_of(part, step)
             if index is None:
                 return
-            g, t = PLACE[index]
-            if t != RUNS[g] - 1:
-                return
-            n = GROUP_BATCHES[g]
-            for j in range(n):
+            if index % RUN == RUN - 1:
                 nc.sync.dma_start(
-                    out=outs[part][FIRST_BATCH[g] + j].rearrange("h (c t) d -> c h (t d)", t=RUNS[g]),
-                    in_=staged[(part, g)][j:P:n].rearrange("p h t d -> p h (t d)"),
+                    out=outs[part][index // RUN].rearrange("h (c t) d -> c h (t d)", t=RUN),
+                    in_=staged[(part, index // RUN)][:].rearrange("p h t d -> p h (t d)"),
                 )
 
         project(0)
-        waiting = [(regroup(flip(x_pair(2))), x_words, x_scales, 2 * P)]
-        for step in range(N_STEPS):
-            flips = []
-            if step % 2 == 1 and step + AHEAD < N_TILES:
-                first_tile = step + AHEAD
-                flips = [(flip(x_pair(first_tile)), x_words, x_scales, first_tile * P)]
-            for part in (K, V):
-                if step == (part - 1) * LAG:
-                    flips = [(flip(w_pair(first)), w_words, w_scales, first) for first in w_pairs[part]]
+        due = {1: [(regroup(flip(x_pair(2))), x_words, x_scales, 2 * P)]}
+        exponent = keep.tile([P, HEADS], F32, name="exponent")
+        nc.vector.tensor_scalar(
+            out=exponent[:], in0=spread(2 * FEATURES, 64)[:, 0:HEADS], scalar1=MAX_LOG_MUL,
+            scalar2=-2.0 / math.log(2.0), op0=ALU.min, op1=ALU.mult,
+        )
+        nc.gpsimd.tensor_tensor(out=shrink[:], in0=two[:], in1=exponent[:], op=ALU.pow)
+        nc.scalar.copy(out=bias_all[V][:], in_=spread(FEATURES, FEATURES)[:])
 
+        for step in range(N_STEPS):
+            flipped_x, flipped_w = None, []
+            if step % 2 == 1 and step + AHEAD < N_TILES:
+                flipped_x = flip(x_pair(step + AHEAD))
+            for part in (K, V):
+                if step == (LAG[part] - 1) // 2 * 2:
+                    flipped_w = [(flip(w_pair(first)), first) for first in w_pairs[part]]
+
+            for tile_pair, words, scales, first in due.get(step, []):
+                quantise(tile_pair, words, scales, first)
             add_bias(Q, step)
-            norms(K, step)
+            q_shrink(step - 2)
+            k_norms(step, range(0, 6))
+            q_gains(step - 2)
+            k_norms(step, range(6, HEADS))
+            q_scale(step - 2)
+            store(Q, step - 2)
             add_bias(V, step)
             store(V, step)
             k_scale(step - 1)
             store(K, step - 1)
-            q_shrink(step - 1)
-            for tile_pair, words, scales, first in waiting:
-                quantise(tile_pair, words, scales, first)
+            q_reduce(step - 1)
+            if flipped_x is not None:
+                due[step + 2] = [(regroup(flipped_x), x_words, x_scales, (step + AHEAD) * P)]
+            grouped_w = [(regroup(bank, nc.vector.tensor_copy), first) for bank, first in flipped_w]
+            for tile_pair, first in grouped_w:
+                quantise(tile_pair, w_words, w_scales, first)
             project(step + 1)
-            waiting = [(regroup(bank), words, scales, first) for bank, words, scales, first in flips]
             k_relu(step)
-            norms(Q, step)
-            q_scale(step - 2)
-            store(Q, step - 2)
+            q_norms(step)
             k_gains(step)
-            q_gains(step - 1)

@@ -25,9 +25,8 @@ EPS = 1e-12
 RUN = TOKENS // P
 N_TILES = BATCHES * RUN
 PART_TILES = FEATURES // P
-AHEAD = 3
 WIDE = 5
-LAG = {Q: 0, K: 1, V: 4}
+LAG = {Q: 0, K: 1, V: 2}
 N_STEPS = N_TILES + LAG[V]
 
 FLOPS = 2 * BATCHES * TOKENS * FEATURES * PARTS * FEATURES
@@ -42,7 +41,7 @@ def tile_selfattention_pa_t_kernel(
         ctx.enter_context(tc.manual_schedule())
         keep = ctx.enter_context(tc.tile_pool(name="keep", bufs=1))
         work = ctx.enter_context(tc.tile_pool(name="work", bufs=3))
-        small = ctx.enter_context(tc.tile_pool(name="small", bufs=4))
+        small = ctx.enter_context(tc.tile_pool(name="small", bufs=6))
         stage = ctx.enter_context(tc.tile_pool(name="stage", bufs=3))
         psum = ctx.enter_context(tc.psum_pool(name="psum", bufs=1))
         banks = {"flipped": 2, "acc0": 2, "acc1": 3, "acc2": 1}
@@ -83,7 +82,7 @@ def tile_selfattention_pa_t_kernel(
         nc.scalar.activation(out=table[:, 1:2], in_=table[:, 0:1], func=ACT.Abs_reciprocal_sqrt)
         ones = keep.tile([P, P], BF16, name="ones")
         nc.vector.memset(ones[:], 1.0)
-        shrink = keep.tile([P, HEADS], F32, name="shrink")
+        multiplier = keep.tile([P, HEADS], F32, name="multiplier")
         floor = keep.tile([P, 2], F32, name="floor")
         nc.vector.memset(floor[:, 0:1], -EPS * EPS)
         nc.vector.memset(floor[:, 1:2], EPS * EPS)
@@ -94,9 +93,8 @@ def tile_selfattention_pa_t_kernel(
         load_x(0, pieces=2)
         load_vectors()
         load_w(K)
-        load_x(1)
         load_w(V)
-        for batch in range(2, BATCHES):
+        for batch in range(1, BATCHES):
             load_x(batch)
 
         w_words = keep.tile([P, PARTS * FEATURES], U32, name="w_words", align_bytes=64)
@@ -104,24 +102,27 @@ def tile_selfattention_pa_t_kernel(
         x_words = keep.tile([P, N_TILES * P], U32, name="x_words", align_bytes=64)
         x_scales = keep.tile([P, N_TILES * P], U8, name="x_scales", align_bytes=64)
 
-        def flip(raw_words):
-            flipped = psum.tile([P, 4 * P], F32, tag="flipped", bufs=banks["flipped"])
+        def flip(raw_words, tag="flipped"):
+            flipped = psum.tile([P, 4 * P], F32, tag=tag, bufs=banks[tag])
             for piece in range(4):
                 cols = slice(piece * P, (piece + 1) * P)
                 j, u = divmod(piece, 2)
                 nc.tensor.transpose(flipped[:, cols], raw_words[:, j * WORDS + u : (j + 1) * WORDS : 2], ident[:])
             return flipped
 
-        def regroup(flipped, copy=nc.scalar.copy):
-            grouped = work.tile([P, 8 * P], BF16, tag="grouped", align_bytes=64)
+        def regroup(flipped, grouped, copy=nc.scalar.copy):
             copy(
-                out=grouped[:].bitcast(F32).rearrange("p (j r u) -> p j r u", j=2, u=2),
+                out=grouped.bitcast(F32).rearrange("p (j r u) -> p j r u", j=2, u=2),
                 in_=flipped[:].rearrange("p (j u r) -> p j r u", j=2, u=2),
             )
+
+        def regroup_pair(flipped, copy=nc.scalar.copy):
+            grouped = work.tile([P, 8 * P], BF16, name="grouped", tag="grouped", align_bytes=64, bufs=4)
+            regroup(flipped, grouped[:], copy)
             return grouped
 
-        def quantise(grouped, words, scales, first):
-            cols = slice(first, first + 2 * P)
+        def quantise(grouped, words, scales, first, width=2 * P):
+            cols = slice(first, first + width)
             nc.vector.quantize_mx(out=words[:, cols].bitcast(FP8X4), scales=scales[:, cols], in_=grouped[:])
 
         def w_pair(first):
@@ -133,8 +134,8 @@ def tile_selfattention_pa_t_kernel(
 
         w_pairs = {part: [part * FEATURES + pair * 2 * P for pair in range(PART_TILES // 2)] for part in (Q, K, V)}
         flipped_w = [flip(w_pair(first)) for first in w_pairs[Q]]
-        grouped_w = [regroup(flipped_w[0]), regroup(flipped_w[1], nc.vector.tensor_copy)]
-        grouped_x = regroup(flip(x_pair(0)))
+        grouped_w = [regroup_pair(flipped_w[0]), regroup_pair(flipped_w[1], nc.vector.tensor_copy)]
+        grouped_x = regroup_pair(flip(x_pair(0)))
         for first, tile_pair in zip(w_pairs[Q], grouped_w):
             quantise(tile_pair, w_words, w_scales, first)
 
@@ -153,8 +154,8 @@ def tile_selfattention_pa_t_kernel(
 
         acc = {}
         staged = {}
-        norm2, gain = {}, {}
-        squares, shrunk, above = {}, {}, {}
+        squares = {}
+        norm2, above, inverse = {}, {}, {}
 
         def by_head(ap):
             return ap.rearrange("p (h d) -> p h d", h=HEADS)
@@ -199,41 +200,58 @@ def tile_selfattention_pa_t_kernel(
             unread = work.tile([P, HEAD_DIM], BF16, tag="unread", bufs=8)
             nc.scalar.activation(out=unread[:], in_=squared, func=ACT.Square, accum_out=norm2_cols)
 
-        def k_norms(step, heads):
+        def norms_of(step):
+            if step not in norm2:
+                norm2[step] = small.tile([P, 2 * HEADS], F32, name="norm2", tag="norm2")
+            return norm2[step]
+
+        def k_norms(step):
             if tile_of(K, step) is None:
                 return
-            if heads[0] == 0:
-                norm2[(K, step)] = small.tile([P, HEADS], F32, name="norm2_k", tag="norm2_k")
-            for h in heads:
-                accumulate(norm2[(K, step)][:, h : h + 1], acc[(K, step)][:, h * HEAD_DIM : (h + 1) * HEAD_DIM])
+            for h in range(HEADS):
+                accumulate(
+                    norms_of(step)[:, HEADS + h : HEADS + h + 1], acc[(K, step)][:, h * HEAD_DIM : (h + 1) * HEAD_DIM]
+                )
+
+        def q_squares(step):
+            if tile_of(Q, step) is None:
+                return
+            squares[step] = work.tile([P, WIDE, HEAD_DIM], F32, name="squares", tag="squares", bufs=2)
+            nc.scalar.activation(out=squares[step][:], in_=slot(Q, step)[:, 0:WIDE, :], func=ACT.Square)
 
         def q_norms(step):
             if tile_of(Q, step) is None:
                 return
-            norm2[(Q, step)] = small.tile([P, HEADS], F32, name="norm2_q", tag="norm2_q")
-            squares[step] = work.tile([P, WIDE, HEAD_DIM], F32, name="squares", tag="squares", bufs=2)
-            nc.scalar.activation(out=squares[step][:], in_=slot(Q, step)[:, 0:WIDE, :], func=ACT.Square)
             for h in range(WIDE, HEADS):
-                accumulate(norm2[(Q, step)][:, h : h + 1], slot(Q, step)[:, h, :])
+                accumulate(norms_of(step + 2)[:, h : h + 1], slot(Q, step)[:, h, :])
 
         def q_reduce(step):
             if tile_of(Q, step) is None:
                 return
-            nc.vector.tensor_reduce(out=norm2[(Q, step)][:, 0:WIDE], in_=squares[step][:], axis=AXIS.X, op=ALU.add)
+            nc.vector.tensor_reduce(out=norms_of(step + 2)[:, 0:WIDE], in_=squares[step][:], axis=AXIS.X, op=ALU.add)
 
-        def q_shrink(step):
-            if tile_of(Q, step) is None:
+        def live(step):
+            first = 0 if tile_of(Q, step - 2) is not None else HEADS
+            last = 2 * HEADS if tile_of(K, step) is not None else HEADS
+            return slice(first, last) if first < last else None
+
+        def clamp(step):
+            if live(step) is None:
                 return
-            shrunk[step] = small.tile([P, HEADS], F32, name="shrunk", tag="shrunk")
-            nc.vector.scalar_tensor_tensor(
-                out=shrunk[step][:], in0=norm2[(Q, step)][:], scalar=EPS * EPS, in1=shrink[:], op0=ALU.max, op1=ALU.mult
+            cols = live(step)
+            above[step] = small.tile([P, 2 * HEADS], F32, name="above", tag="above")
+            nc.scalar.activation(
+                out=above[step][:, cols], in_=norm2[step][:, cols], func=ACT.Relu, bias=floor[:, 0:1]
             )
 
-        def q_gains(step):
-            if tile_of(Q, step) is None:
+        def invert(step):
+            if live(step) is None:
                 return
-            gain[(Q, step)] = small.tile([P, HEADS], F32, name="gain_q", tag="gain_q")
-            nc.scalar.activation(out=gain[(Q, step)][:], in_=shrunk[step][:], func=ACT.Abs_reciprocal_sqrt)
+            cols = live(step)
+            inverse[step] = small.tile([P, 2 * HEADS], F32, name="inverse", tag="inverse")
+            nc.scalar.activation(
+                out=inverse[step][:, cols], in_=above[step][:, cols], func=ACT.Abs_reciprocal_sqrt, bias=floor[:, 1:2]
+            )
 
         def over_head(gain_cols):
             return gain_cols.unsqueeze(2).to_broadcast([P, HEADS, HEAD_DIM])
@@ -241,23 +259,9 @@ def tile_selfattention_pa_t_kernel(
         def q_scale(step):
             if tile_of(Q, step) is None:
                 return
-            nc.gpsimd.tensor_tensor(
-                out=slot(Q, step), in0=slot(Q, step), in1=over_head(gain[(Q, step)][:]), op=ALU.mult
-            )
-
-        def k_relu(step):
-            if tile_of(K, step) is None:
-                return
-            above[step] = small.tile([P, HEADS], F32, name="above", tag="above")
-            nc.scalar.activation(out=above[step][:], in_=norm2[(K, step)][:], func=ACT.Relu, bias=floor[:, 0:1])
-
-        def k_gains(step):
-            if tile_of(K, step) is None:
-                return
-            gain[(K, step)] = small.tile([P, HEADS], F32, name="gain_k", tag="gain_k")
-            nc.scalar.activation(
-                out=gain[(K, step)][:], in_=above[step][:], func=ACT.Abs_reciprocal_sqrt, bias=floor[:, 1:2]
-            )
+            gain = small.tile([P, HEADS], F32, name="gain", tag="gain")
+            nc.gpsimd.tensor_tensor(out=gain[:], in0=inverse[step + 2][:, 0:HEADS], in1=multiplier[:], op=ALU.mult)
+            nc.gpsimd.tensor_tensor(out=slot(Q, step), in0=slot(Q, step), in1=over_head(gain[:]), op=ALU.mult)
 
         def k_scale(step):
             if tile_of(K, step) is None:
@@ -265,57 +269,67 @@ def tile_selfattention_pa_t_kernel(
             new_stage(K, step)
             nc.vector.tensor_tensor(
                 out=slot(K, step), in0=by_head(acc[(K, step)][:]),
-                in1=over_head(gain[(K, step)][:]), op=ALU.mult,
+                in1=over_head(inverse[step][:, HEADS : 2 * HEADS]), op=ALU.mult,
             )
 
         def store(part, step):
             index = tile_of(part, step)
             if index is None:
                 return
-            if index % RUN == RUN - 1:
+            batch, t = divmod(index, RUN)
+            size = RUN // 2 if batch in (0, BATCHES - 1) else RUN
+            if (t + 1) % size == 0:
+                cols = slice((t + 1 - size) * HEAD_DIM, (t + 1) * HEAD_DIM)
                 nc.sync.dma_start(
-                    out=outs[part][index // RUN].rearrange("h (c t) d -> c h (t d)", t=RUN),
-                    in_=staged[(part, index // RUN)][:].rearrange("p h t d -> p h (t d)"),
+                    out=outs[part][batch].rearrange("h (c t) d -> c h (t d)", t=RUN)[:, :, cols],
+                    in_=staged[(part, batch)][:].rearrange("p h t d -> p h (t d)")[:, :, cols],
                 )
 
         project(0)
-        due = {1: [(regroup(flip(x_pair(2))), x_words, x_scales, 2 * P)]}
+        grouped_x = regroup_pair(flip(x_pair(2)))
         exponent = keep.tile([P, HEADS], F32, name="exponent")
         nc.vector.tensor_scalar(
             out=exponent[:], in0=spread(2 * FEATURES, 64)[:, 0:HEADS], scalar1=MAX_LOG_MUL,
-            scalar2=-2.0 / math.log(2.0), op0=ALU.min, op1=ALU.mult,
+            scalar2=1.0 / math.log(2.0), op0=ALU.min, op1=ALU.mult,
         )
-        nc.gpsimd.tensor_tensor(out=shrink[:], in0=two[:], in1=exponent[:], op=ALU.pow)
+        nc.gpsimd.tensor_tensor(out=multiplier[:], in0=two[:], in1=exponent[:], op=ALU.pow)
         nc.scalar.copy(out=bias_all[V][:], in_=spread(FEATURES, FEATURES)[:])
 
-        for step in range(N_STEPS):
-            flipped_x, flipped_w = None, []
-            if step % 2 == 1 and step + AHEAD < N_TILES:
-                flipped_x = flip(x_pair(step + AHEAD))
-            for part in (K, V):
-                if step == (LAG[part] - 1) // 2 * 2:
-                    flipped_w = [(flip(w_pair(first)), first) for first in w_pairs[part]]
+        def pack_w(part, tags):
+            flipped_w = [flip(w_pair(first), tag) for first, tag in zip(w_pairs[part], tags)]
+            grouped_w = [regroup_pair(flipped, nc.vector.tensor_copy) for flipped in flipped_w]
+            for first, tile_pair in zip(w_pairs[part], grouped_w):
+                quantise(tile_pair, w_words, w_scales, first)
 
-            for tile_pair, words, scales, first in due.get(step, []):
-                quantise(tile_pair, words, scales, first)
+        flipped_x = {}
+        for step in range(N_STEPS):
+            batch, t = divmod(step, RUN)
+            packs = batch + 1 < BATCHES
+            if packs and t == 0:
+                first_tile = (batch + 1) * RUN
+                flipped_x = {step: flip(x_pair(first_tile)), step + 1: flip(x_pair(first_tile + 2))}
+                grouped_batch = work.tile([P, 16 * P], BF16, name="grouped_batch", align_bytes=64, bufs=2)
+
             add_bias(Q, step)
-            q_shrink(step - 2)
-            k_norms(step, range(0, 6))
-            q_gains(step - 2)
-            k_norms(step, range(6, HEADS))
-            q_scale(step - 2)
-            store(Q, step - 2)
+            k_norms(step)
             add_bias(V, step)
             store(V, step)
             k_scale(step - 1)
             store(K, step - 1)
+            if packs and t in (0, 1):
+                regroup(flipped_x[step], grouped_batch[:, t * 8 * P : (t + 1) * 8 * P])
+            if packs and t == 2:
+                quantise(grouped_batch, x_words, x_scales, (batch + 1) * RUN * P, width=RUN * P)
             q_reduce(step - 1)
-            if flipped_x is not None:
-                due[step + 2] = [(regroup(flipped_x), x_words, x_scales, (step + AHEAD) * P)]
-            grouped_w = [(regroup(bank, nc.vector.tensor_copy), first) for bank, first in flipped_w]
-            for tile_pair, first in grouped_w:
-                quantise(tile_pair, w_words, w_scales, first)
-            project(step + 1)
-            k_relu(step)
+            clamp(step)
+            q_squares(step)
+            invert(step)
             q_norms(step)
-            k_gains(step)
+            q_scale(step - 2)
+            store(Q, step - 2)
+            if step == 0:
+                quantise(grouped_x, x_words, x_scales, 2 * P)
+                pack_w(K, ("acc1", "acc1"))
+            project(step + 1)
+            if step == 0:
+                pack_w(V, ("acc1", "acc2"))

@@ -25,9 +25,9 @@ EPS = 1e-12
 RUN = TOKENS // P
 N_TILES = BATCHES * RUN
 PART_TILES = FEATURES // P
-WIDE = 5
-LAG = {Q: 0, K: 1, V: 2}
-N_STEPS = N_TILES + LAG[V]
+WIDE = 6
+LAG = {Q: 0, V: 1, K: 2}
+N_STEPS = N_TILES + LAG[K] + 1
 
 FLOPS = 2 * BATCHES * TOKENS * FEATURES * PARTS * FEATURES
 
@@ -92,8 +92,8 @@ def tile_selfattention_pa_t_kernel(
         load_w(Q, halves=2)
         load_x(0, pieces=2)
         load_vectors()
-        load_w(K)
         load_w(V)
+        load_w(K)
         for batch in range(1, BATCHES):
             load_x(batch)
 
@@ -133,11 +133,19 @@ def tile_selfattention_pa_t_kernel(
             return x_raw[batch][:].bitcast(F32)[:, t * WORDS : (t + 2) * WORDS]
 
         w_pairs = {part: [part * FEATURES + pair * 2 * P for pair in range(PART_TILES // 2)] for part in (Q, K, V)}
-        flipped_w = [flip(w_pair(first)) for first in w_pairs[Q]]
+
+        def flip_w(part, tag):
+            return [flip(w_pair(first), tag) for first in w_pairs[part]]
+
+        def quantise_w(part, grouped_w):
+            for first, grouped in zip(w_pairs[part], grouped_w):
+                quantise(grouped, w_words, w_scales, first)
+
+        flipped_w = flip_w(Q, "flipped")
         grouped_w = [regroup_pair(flipped_w[0]), regroup_pair(flipped_w[1], nc.vector.tensor_copy)]
         grouped_x = regroup_pair(flip(x_pair(0)))
-        for first, tile_pair in zip(w_pairs[Q], grouped_w):
-            quantise(tile_pair, w_words, w_scales, first)
+        quantise_w(Q, grouped_w)
+        quantise(grouped_x, x_words, x_scales, 0)
 
         def spread(first, width):
             acc = psum.tile([P, FEATURES], F32, tag="acc1", bufs=banks["acc1"])
@@ -145,8 +153,13 @@ def tile_selfattention_pa_t_kernel(
             return acc
 
         bias_all = {part: keep.tile([P, FEATURES], F32, name="bias_all%d" % part) for part in (Q, V)}
-        quantise(grouped_x, x_words, x_scales, 0)
         nc.scalar.copy(out=bias_all[Q][:], in_=spread(0, FEATURES)[:])
+        exponent = keep.tile([P, HEADS], F32, name="exponent")
+        nc.vector.tensor_scalar(
+            out=exponent[:], in0=spread(2 * FEATURES, 64)[:, 0:HEADS], scalar1=MAX_LOG_MUL,
+            scalar2=1.0 / math.log(2.0), op0=ALU.min, op1=ALU.mult,
+        )
+        nc.gpsimd.tensor_tensor(out=multiplier[:], in0=two[:], in1=exponent[:], op=ALU.pow)
 
         def tile_of(part, step):
             index = step - LAG[part]
@@ -277,7 +290,7 @@ def tile_selfattention_pa_t_kernel(
             if index is None:
                 return
             batch, t = divmod(index, RUN)
-            size = RUN // 2 if batch in (0, BATCHES - 1) else RUN
+            size = RUN // 2 if batch == 0 else RUN
             if (t + 1) % size == 0:
                 cols = slice((t + 1 - size) * HEAD_DIM, (t + 1) * HEAD_DIM)
                 nc.sync.dma_start(
@@ -286,29 +299,20 @@ def tile_selfattention_pa_t_kernel(
                 )
 
         project(0)
+        flipped_w = flip_w(V, "acc%d" % K)
         grouped_x = regroup_pair(flip(x_pair(2)))
-        exponent = keep.tile([P, HEADS], F32, name="exponent")
-        nc.vector.tensor_scalar(
-            out=exponent[:], in0=spread(2 * FEATURES, 64)[:, 0:HEADS], scalar1=MAX_LOG_MUL,
-            scalar2=1.0 / math.log(2.0), op0=ALU.min, op1=ALU.mult,
-        )
-        nc.gpsimd.tensor_tensor(out=multiplier[:], in0=two[:], in1=exponent[:], op=ALU.pow)
         nc.scalar.copy(out=bias_all[V][:], in_=spread(FEATURES, FEATURES)[:])
 
-        def pack_w(part, tags):
-            flipped_w = [flip(w_pair(first), tag) for first, tag in zip(w_pairs[part], tags)]
-            grouped_w = [regroup_pair(flipped, nc.vector.tensor_copy) for flipped in flipped_w]
-            for first, tile_pair in zip(w_pairs[part], grouped_w):
-                quantise(tile_pair, w_words, w_scales, first)
+        def flip_batch(batch):
+            return [flip(x_pair(batch * RUN + first)) for first in range(0, RUN, 2)]
 
-        flipped_x = {}
         for step in range(N_STEPS):
             batch, t = divmod(step, RUN)
             packs = batch + 1 < BATCHES
-            if packs and t == 0:
-                first_tile = (batch + 1) * RUN
-                flipped_x = {step: flip(x_pair(first_tile)), step + 1: flip(x_pair(first_tile + 2))}
-                grouped_batch = work.tile([P, 16 * P], BF16, name="grouped_batch", align_bytes=64, bufs=2)
+            if packs and t == 0 and step > 0:
+                flipped_x = flip_batch(batch + 1)
+            if step == 1:
+                quantise(grouped_x, x_words, x_scales, 2 * P)
 
             add_bias(Q, step)
             k_norms(step)
@@ -316,8 +320,18 @@ def tile_selfattention_pa_t_kernel(
             store(V, step)
             k_scale(step - 1)
             store(K, step - 1)
+            if step == 0:
+                quantise_w(V, [regroup_pair(flipped, nc.vector.tensor_copy) for flipped in flipped_w])
+            if step == 1:
+                quantise_w(K, grouped_w)
+            project(step + 1)
+            if step == 0:
+                grouped_w = [regroup_pair(flipped) for flipped in flip_w(K, "acc%d" % K)]
+                flipped_x = flip_batch(1)
+            if packs and t == 0:
+                grouped_batch = work.tile([P, 16 * P], BF16, name="grouped_batch", align_bytes=64, bufs=2)
             if packs and t in (0, 1):
-                regroup(flipped_x[step], grouped_batch[:, t * 8 * P : (t + 1) * 8 * P])
+                regroup(flipped_x[t], grouped_batch[:, t * 8 * P : (t + 1) * 8 * P])
             if packs and t == 2:
                 quantise(grouped_batch, x_words, x_scales, (batch + 1) * RUN * P, width=RUN * P)
             q_reduce(step - 1)
@@ -327,9 +341,3 @@ def tile_selfattention_pa_t_kernel(
             q_norms(step)
             q_scale(step - 2)
             store(Q, step - 2)
-            if step == 0:
-                quantise(grouped_x, x_words, x_scales, 2 * P)
-                pack_w(K, ("acc1", "acc1"))
-            project(step + 1)
-            if step == 0:
-                pack_w(V, ("acc1", "acc2"))

import math
from contextlib import ExitStack

import concourse.mybir as mybir
from concourse.masks import make_identity

F32 = mybir.dt.float32
BF16 = mybir.dt.bfloat16
U32 = mybir.dt.uint32
U8 = mybir.dt.uint8
FP8X4 = mybir.dt.float8_e4m3fn_x4
ALU = mybir.AluOpType
ACT = mybir.ActivationFunctionType
AXIS = mybir.AxisListType

P = 128
BATCHES, TOKENS, FEATURES, HEADS = 8, 512, 512, 8
HEAD_DIM = FEATURES // HEADS
WORDS = FEATURES // 2
PARTS = 3
Q, K, V = 0, 1, 2
MAX_LOG_MUL = math.log(100.0)
EPS = 1e-12

RUN = TOKENS // P
N_TILES = BATCHES * RUN
PART_TILES = FEATURES // P
WIDE = 6
LAG = {Q: 0, V: 1, K: 2}
N_STEPS = N_TILES + LAG[K] + 1

FLOPS = 2 * BATCHES * TOKENS * FEATURES * PARTS * FEATURES


def tile_selfattention_pa_t_kernel(
    tc, x, w_qkv, q_bias, v_bias, log_scale_mul, out_q, out_k, out_v
):
    nc = tc.nc
    outs = [out_q, out_k, out_v]
    with ExitStack() as ctx:
        ctx.enter_context(tc.manual_schedule())
        keep = ctx.enter_context(tc.tile_pool(name="keep", bufs=1))
        work = ctx.enter_context(tc.tile_pool(name="work", bufs=3))
        small = ctx.enter_context(tc.tile_pool(name="small", bufs=6))
        stage = ctx.enter_context(tc.tile_pool(name="stage", bufs=3))
        psum = ctx.enter_context(tc.psum_pool(name="psum", bufs=1))
        banks = {"flipped": 2, "acc0": 2, "acc1": 3, "acc2": 1}

        w_raw = keep.tile([P, PARTS * PART_TILES * FEATURES], BF16, name="w_raw")
        x_raw = [keep.tile([P, RUN * FEATURES], BF16, name="x_raw%d" % b) for b in range(BATCHES)]
        rows = keep.tile([P, 2 * FEATURES + 64], BF16, name="rows")

        def load_w(part, halves=1):
            tiles = PART_TILES // halves
            for first in range(part * PART_TILES, (part + 1) * PART_TILES, tiles):
                nc.sync.dma_start(
                    out=w_raw[:, first * FEATURES : (first + tiles) * FEATURES].rearrange("p (n f) -> p n f", n=tiles),
                    in_=w_qkv[first * P : (first + tiles) * P, :].rearrange("(n p) f -> p n f", p=P),
                )

        def load_x(batch, pieces=1):
            width = RUN * FEATURES // pieces
            for piece in range(pieces):
                cols = slice(piece * width, (piece + 1) * width)
                nc.sync.dma_start(
                    out=x_raw[batch][:, cols], in_=x[batch].rearrange("(c t) f -> c (t f)", t=RUN)[:, cols]
                )

        def load_vectors():
            nc.sync.dma_start(out=rows[0:1, 0:FEATURES], in_=q_bias.rearrange("(o n) -> o n", o=1))
            nc.sync.dma_start(
                out=rows[0:1, 2 * FEATURES : 2 * FEATURES + HEADS],
                in_=log_scale_mul.rearrange("a h b c -> a (h b c)"),
            )
            nc.sync.dma_start(out=rows[0:1, FEATURES : 2 * FEATURES], in_=v_bias.rearrange("(o n) -> o n", o=1))

        ident = keep.tile([P, P], F32, name="ident")
        make_identity(nc, ident[:])
        nc.gpsimd.memset(rows[:].bitcast(F32), 0.0)
        table = keep.tile([P, 2], F32, name="table")
        nc.vector.memset(table[:, 0:1], 1.0)
        nc.scalar.activation(out=table[:, 1:2], in_=table[:, 0:1], func=ACT.Abs_reciprocal_sqrt)
        ones = keep.tile([P, P], BF16, name="ones")
        nc.vector.memset(ones[:], 1.0)
        multiplier = keep.tile([P, HEADS], F32, name="multiplier")
        floor = keep.tile([P, 2], F32, name="floor")
        nc.vector.memset(floor[:, 0:1], -EPS * EPS)
        nc.vector.memset(floor[:, 1:2], EPS * EPS)
        two = keep.tile([P, HEADS], F32, name="two")
        nc.vector.memset(two[:], 2.0)

        load_w(Q, halves=2)
        load_x(0, pieces=2)
        load_vectors()
        load_w(V)
        load_w(K)
        for batch in range(1, BATCHES):
            load_x(batch)

        w_words = keep.tile([P, PARTS * FEATURES], U32, name="w_words", align_bytes=64)
        w_scales = keep.tile([P, PARTS * FEATURES], U8, name="w_scales", align_bytes=64)
        x_words = keep.tile([P, N_TILES * P], U32, name="x_words", align_bytes=64)
        x_scales = keep.tile([P, N_TILES * P], U8, name="x_scales", align_bytes=64)

        def flip(raw_words, tag="flipped"):
            flipped = psum.tile([P, 4 * P], F32, tag=tag, bufs=banks[tag])
            for piece in range(4):
                cols = slice(piece * P, (piece + 1) * P)
                j, u = divmod(piece, 2)
                nc.tensor.transpose(flipped[:, cols], raw_words[:, j * WORDS + u : (j + 1) * WORDS : 2], ident[:])
            return flipped

        def regroup(flipped, grouped, copy=nc.scalar.copy):
            copy(
                out=grouped.bitcast(F32).rearrange("p (j r u) -> p j r u", j=2, u=2),
                in_=flipped[:].rearrange("p (j u r) -> p j r u", j=2, u=2),
            )

        def regroup_pair(flipped, copy=nc.scalar.copy):
            grouped = work.tile([P, 8 * P], BF16, name="grouped", tag="grouped", align_bytes=64, bufs=4)
            regroup(flipped, grouped[:], copy)
            return grouped

        def quantise(grouped, words, scales, first, width=2 * P):
            cols = slice(first, first + width)
            nc.vector.quantize_mx(out=words[:, cols].bitcast(FP8X4), scales=scales[:, cols], in_=grouped[:])

        def w_pair(first):
            return w_raw[:].bitcast(F32)[:, first * WORDS // P : (first + 2 * P) * WORDS // P]

        def x_pair(first_tile):
            batch, t = divmod(first_tile, RUN)
            return x_raw[batch][:].bitcast(F32)[:, t * WORDS : (t + 2) * WORDS]

        w_pairs = {part: [part * FEATURES + pair * 2 * P for pair in range(PART_TILES // 2)] for part in (Q, K, V)}

        def flip_w(part, tag):
            return [flip(w_pair(first), tag) for first in w_pairs[part]]

        def quantise_w(part, grouped_w):
            for first, grouped in zip(w_pairs[part], grouped_w):
                quantise(grouped, w_words, w_scales, first)

        flipped_w = flip_w(Q, "flipped")
        grouped_w = [regroup_pair(flipped_w[0]), regroup_pair(flipped_w[1], nc.vector.tensor_copy)]
        grouped_x = regroup_pair(flip(x_pair(0)))
        quantise_w(Q, grouped_w)
        quantise(grouped_x, x_words, x_scales, 0)

        def spread(first, width):
            acc = psum.tile([P, FEATURES], F32, tag="acc1", bufs=banks["acc1"])
            nc.tensor.matmul(acc[:, 0:width], lhsT=ones[:], rhs=rows[:, first : first + width], start=True, stop=True)
            return acc

        bias_all = {part: keep.tile([P, FEATURES], F32, name="bias_all%d" % part) for part in (Q, V)}
        nc.scalar.copy(out=bias_all[Q][:], in_=spread(0, FEATURES)[:])
        exponent = keep.tile([P, HEADS], F32, name="exponent")
        nc.vector.tensor_scalar(
            out=exponent[:], in0=spread(2 * FEATURES, 64)[:, 0:HEADS], scalar1=MAX_LOG_MUL,
            scalar2=1.0 / math.log(2.0), op0=ALU.min, op1=ALU.mult,
        )
        nc.gpsimd.tensor_tensor(out=multiplier[:], in0=two[:], in1=exponent[:], op=ALU.pow)

        def tile_of(part, step):
            index = step - LAG[part]
            return index if 0 <= index < N_TILES else None

        acc = {}
        staged = {}
        squares = {}
        norm2, above, inverse = {}, {}, {}

        def by_head(ap):
            return ap.rearrange("p (h d) -> p h d", h=HEADS)

        def slot(part, step):
            batch, t = divmod(tile_of(part, step), RUN)
            return staged[(part, batch)][:, :, t, :]

        def project(step):
            for part in (Q, K, V):
                index = tile_of(part, step)
                if index is None:
                    continue
                bank = psum.tile([P, FEATURES], F32, tag="acc%d" % part, bufs=banks["acc%d" % part])
                nc.tensor.matmul_mx(
                    out=bank[:],
                    lhsT=x_words[:, index * P : (index + 1) * P].bitcast(FP8X4),
                    lhsT_scale=x_scales[:, index * P : (index + 1) * P],
                    rhs=w_words[:, part * FEATURES : (part + 1) * FEATURES].bitcast(FP8X4),
                    rhs_scale=w_scales[:, part * FEATURES : (part + 1) * FEATURES],
                    start=True,
                    stop=True,
                )
                acc[(part, step)] = bank

        def new_stage(part, step):
            index = tile_of(part, step)
            if index is not None and index % RUN == 0:
                staged[(part, index // RUN)] = stage.tile(
                    [P, HEADS, RUN, HEAD_DIM], F32, name="staged%d" % part, tag="staged%d" % part
                )

        def add_bias(part, step):
            if tile_of(part, step) is None:
                return
            new_stage(part, step)
            nc.vector.tensor_tensor(
                out=slot(part, step), in0=by_head(acc[(part, step)][:]), in1=by_head(bias_all[part][:]), op=ALU.add
            )

        def accumulate(norm2_cols, squared):
            unread = work.tile([P, HEAD_DIM], BF16, tag="unread", bufs=8)
            nc.scalar.activation(out=unread[:], in_=squared, func=ACT.Square, accum_out=norm2_cols)

        def norms_of(step):
            if step not in norm2:
                norm2[step] = small.tile([P, 2 * HEADS], F32, name="norm2", tag="norm2")
            return norm2[step]

        def k_norms(step):
            if tile_of(K, step) is None:
                return
            for h in range(HEADS):
                accumulate(
                    norms_of(step)[:, HEADS + h : HEADS + h + 1], acc[(K, step)][:, h * HEAD_DIM : (h + 1) * HEAD_DIM]
                )

        def q_squares(step):
            if tile_of(Q, step) is None:
                return
            squares[step] = work.tile([P, WIDE, HEAD_DIM], F32, name="squares", tag="squares", bufs=2)
            nc.scalar.activation(out=squares[step][:], in_=slot(Q, step)[:, 0:WIDE, :], func=ACT.Square)

        def q_norms(step):
            if tile_of(Q, step) is None:
                return
            for h in range(WIDE, HEADS):
                accumulate(norms_of(step + 2)[:, h : h + 1], slot(Q, step)[:, h, :])

        def q_reduce(step):
            if tile_of(Q, step) is None:
                return
            nc.vector.tensor_reduce(out=norms_of(step + 2)[:, 0:WIDE], in_=squares[step][:], axis=AXIS.X, op=ALU.add)

        def live(step):
            first = 0 if tile_of(Q, step - 2) is not None else HEADS
            last = 2 * HEADS if tile_of(K, step) is not None else HEADS
            return slice(first, last) if first < last else None

        def clamp(step):
            if live(step) is None:
                return
            cols = live(step)
            above[step] = small.tile([P, 2 * HEADS], F32, name="above", tag="above")
            nc.scalar.activation(
                out=above[step][:, cols], in_=norm2[step][:, cols], func=ACT.Relu, bias=floor[:, 0:1]
            )

        def invert(step):
            if live(step) is None:
                return
            cols = live(step)
            inverse[step] = small.tile([P, 2 * HEADS], F32, name="inverse", tag="inverse")
            nc.scalar.activation(
                out=inverse[step][:, cols], in_=above[step][:, cols], func=ACT.Abs_reciprocal_sqrt, bias=floor[:, 1:2]
            )

        def over_head(gain_cols):
            return gain_cols.unsqueeze(2).to_broadcast([P, HEADS, HEAD_DIM])

        def q_scale(step):
            if tile_of(Q, step) is None:
                return
            gain = small.tile([P, HEADS], F32, name="gain", tag="gain")
            nc.gpsimd.tensor_tensor(out=gain[:], in0=inverse[step + 2][:, 0:HEADS], in1=multiplier[:], op=ALU.mult)
            nc.gpsimd.tensor_tensor(out=slot(Q, step), in0=slot(Q, step), in1=over_head(gain[:]), op=ALU.mult)

        def k_scale(step):
            if tile_of(K, step) is None:
                return
            new_stage(K, step)
            nc.vector.tensor_tensor(
                out=slot(K, step), in0=by_head(acc[(K, step)][:]),
                in1=over_head(inverse[step][:, HEADS : 2 * HEADS]), op=ALU.mult,
            )

        def store(part, step):
            index = tile_of(part, step)
            if index is None:
                return
            batch, t = divmod(index, RUN)
            size = RUN // 2 if batch == 0 else RUN
            if (t + 1) % size == 0:
                cols = slice((t + 1 - size) * HEAD_DIM, (t + 1) * HEAD_DIM)
                nc.sync.dma_start(
                    out=outs[part][batch].rearrange("h (c t) d -> c h (t d)", t=RUN)[:, :, cols],
                    in_=staged[(part, batch)][:].rearrange("p h t d -> p h (t d)")[:, :, cols],
                )

        project(0)
        flipped_w = flip_w(V, "acc%d" % K)
        grouped_x = regroup_pair(flip(x_pair(2)))
        nc.scalar.copy(out=bias_all[V][:], in_=spread(FEATURES, FEATURES)[:])

        def flip_batch(batch):
            return [flip(x_pair(batch * RUN + first)) for first in range(0, RUN, 2)]

        for step in range(N_STEPS):
            batch, t = divmod(step, RUN)
            packs = batch + 1 < BATCHES
            if packs and t == 0 and step > 0:
                flipped_x = flip_batch(batch + 1)
            if step == 1:
                quantise(grouped_x, x_words, x_scales, 2 * P)

            add_bias(Q, step)
            k_norms(step)
            add_bias(V, step)
            store(V, step)
            k_scale(step - 1)
            store(K, step - 1)
            if step == 0:
                quantise_w(V, [regroup_pair(flipped, nc.vector.tensor_copy) for flipped in flipped_w])
            if step == 1:
                quantise_w(K, grouped_w)
            project(step + 1)
            if step == 0:
                grouped_w = [regroup_pair(flipped) for flipped in flip_w(K, "acc%d" % K)]
                flipped_x = flip_batch(1)
            if packs and t == 0:
                grouped_batch = work.tile([P, 16 * P], BF16, name="grouped_batch", align_bytes=64, bufs=2)
            if packs and t in (0, 1):
                regroup(flipped_x[t], grouped_batch[:, t * 8 * P : (t + 1) * 8 * P])
            if packs and t == 2:
                quantise(grouped_batch, x_words, x_scales, (batch + 1) * RUN * P, width=RUN * P)
            q_reduce(step - 1)
            clamp(step)
            q_squares(step)
            invert(step)
            q_norms(step)
            q_scale(step - 2)
            store(Q, step - 2)
